import numpy as np
import ml_dtypes

BF16 = ml_dtypes.bfloat16


def bf(x):
    return np.asarray(x, np.float32).astype(BF16)


def f32(x):
    return np.asarray(x, np.float32)


def f64(x):
    return np.asarray(x).astype(np.float64)


def striped(idx):
    return np.tile(idx.reshape(-1, 16).T, (8, 1))


C, S, K, Q, L, N = 1024, 256, 6, 16, 8, 128
KAPPA, BETA_GROUP = 6.0, 6.0


def sigmoid(v):
    return 1.0 / (1.0 + np.exp(-v))


def setup_inputs():
    return {"x": f32(np.random.standard_normal((C, S))), "th": f32(0.5 * np.random.standard_normal((K, N))), "ineq": f32(0.5 * np.random.standard_normal((K, N))), "esign": f32(np.random.standard_normal((K, N))), "mask": f32(np.random.standard_normal((K, N))), "tau": f32(0.3 * np.random.standard_normal((K, Q))), "offs": striped(np.random.permutation(S)[:N])}


def reference(x, th, ineq, esign, mask, tau, offs):
    idx = offs[:16].T.reshape(-1)
    nth = -f64(th)
    d = f64(x)[:, idx][:, None, :] + nth[None]
    c = sigmoid(KAPPA * np.tanh(f64(ineq))[None] * d)
    a = sigmoid(f64(mask)) * np.tanh(f64(esign))
    sym = a[None] * (2.0 * c - 1.0)
    eg = sym.reshape(C, K, Q, L).sum(axis=-1)
    return sigmoid(BETA_GROUP * (eg - f64(tau)[None])).reshape(C, K * Q)

@@ -1,0 +1,73 @@
+import concourse.mybir as mybir
+
+F32 = mybir.dt.float32
+U16 = mybir.dt.uint16
+ADD = mybir.AluOpType.add
+MULT = mybir.AluOpType.mult
+SUBTRACT = mybir.AluOpType.subtract
+FUNC = mybir.ActivationFunctionType
+
+P = 128
+C, S, K, Q, L, N = 1024, 256, 6, 16, 8, 128
+KN = K * N
+KQ = K * Q
+BLOCKS = C // P
+
+
+def tile_regimerulesnet_kernel(tc, x, th, ineq, esign, mask, tau, offs, out):
+    nc = tc.nc
+    with (
+        tc.tile_pool(name="held", bufs=1) as held,
+        tc.tile_pool(name="work", bufs=2) as work,
+    ):
+        offsets = held.tile([P, N // 16], U16, name="offsets")
+        nc.sync.dma_start(offsets[:], offs)
+
+        th_all = held.tile([P, KN], F32, name="th_all")
+        ineq_all = held.tile([P, KN], F32, name="ineq_all")
+        esign_all = held.tile([P, KN], F32, name="esign_all")
+        mask_all = held.tile([P, KN], F32, name="mask_all")
+        tau_all = held.tile([P, KQ], F32, name="tau_all")
+        nc.scalar.dma_start(th_all[:], th.rearrange("k n -> (k n)").partition_broadcast(P))
+        nc.gpsimd.dma_start(ineq_all[:], ineq.rearrange("k n -> (k n)").partition_broadcast(P))
+        nc.scalar.dma_start(esign_all[:], esign.rearrange("k n -> (k n)").partition_broadcast(P))
+        nc.gpsimd.dma_start(mask_all[:], mask.rearrange("k n -> (k n)").partition_broadcast(P))
+        nc.gpsimd.dma_start(tau_all[:], tau.rearrange("k q -> (k q)").partition_broadcast(P))
+
+        x_blocks = []
+        for b in range(BLOCKS):
+            x_block = held.tile([P, S], F32, name=f"x_block{b}")
+            nc.sync.dma_start(x_block[:], x[b * P : (b + 1) * P, :])
+            x_blocks.append(x_block)
+
+        nth = held.tile([P, KN], F32, name="nth")
+        nc.vector.tensor_scalar_mul(nth[:], th_all[:], -1.0)
+        slope = held.tile([P, KN], F32, name="slope")
+        nc.scalar.activation(slope[:], ineq_all[:], FUNC.Tanh)
+        sign = held.tile([P, KN], F32, name="sign")
+        nc.scalar.activation(sign[:], esign_all[:], FUNC.Tanh)
+        gate = held.tile([P, KN], F32, name="gate")
+        nc.scalar.activation(gate[:], mask_all[:], FUNC.Sigmoid)
+        a = held.tile([P, KN], F32, name="a")
+        nc.gpsimd.tensor_tensor(a[:], gate[:], sign[:], MULT)
+
+        for b in range(BLOCKS):
+            d = work.tile([P, KN], F32, name="d")
+            for k in range(K):
+                regime = slice(k * N, (k + 1) * N)
+                nc.vector.tensor_tensor(d[:, regime], x_blocks[b][:].indirect(offsets[:]), nth[:, regime], ADD)
+            steep = work.tile([P, KN], F32, name="steep")
+            nc.gpsimd.tensor_tensor(steep[:], d[:], slope[:], MULT)
+            rule = work.tile([P, KN], F32, name="rule")
+            nc.scalar.activation(rule[:], steep[:], FUNC.Tanh, scale=3.0)
+            evidence = work.tile([P, KN], F32, name="evidence")
+            nc.gpsimd.tensor_tensor(evidence[:], rule[:], a[:], MULT)
+            eg = work.tile([P, KQ], F32, name="eg")
+            nc.vector.tensor_reduce(
+                eg[:], evidence[:].rearrange("p (g l) -> p g l", l=L), axis=mybir.AxisListType.X, op=ADD
+            )
+            margin = work.tile([P, KQ], F32, name="margin")
+            nc.vector.tensor_tensor(margin[:], eg[:], tau_all[:], SUBTRACT)
+            active = work.tile([P, KQ], F32, name="active")
+            nc.scalar.activation(active[:], margin[:], FUNC.Sigmoid, scale=6.0)
+            nc.sync.dma_start(out[b * P : (b + 1) * P, :], active[:])

@@ -1,10 +1,12 @@
 import concourse.mybir as mybir
+from concourse.masks import make_identity
 
 F32 = mybir.dt.float32
+BF16 = mybir.dt.bfloat16
 U16 = mybir.dt.uint16
 ADD = mybir.AluOpType.add
 MULT = mybir.AluOpType.mult
-SUBTRACT = mybir.AluOpType.subtract
+IS_GE = mybir.AluOpType.is_ge
 FUNC = mybir.ActivationFunctionType
 
 P = 128
@@ -12,62 +14,124 @@ C, S, K, Q, L, N = 1024, 256, 6, 16, 8, 128
 KN = K * N
 KQ = K * Q
 BLOCKS = C // P
+TEAM = 4
+TEAMS = BLOCKS // TEAM
+STEPS = TEAMS * K
+SUM_DT = BF16
+FLOPS = 2 * C * K * N
 
 
 def tile_regimerulesnet_kernel(tc, x, th, ineq, esign, mask, tau, offs, out):
     nc = tc.nc
+    x_view = x.rearrange("(p b) s -> p b s", b=BLOCKS)
+    out_view = out.rearrange("(p b) f -> p b f", b=BLOCKS)
     with (
         tc.tile_pool(name="held", bufs=1) as held,
-        tc.tile_pool(name="work", bufs=2) as work,
+        tc.tile_pool(name="d_pool", bufs=3 * TEAM) as d_pool,
+        tc.tile_pool(name="rule_pool", bufs=3 * TEAM) as rule_pool,
+        tc.tile_pool(name="out_pool", bufs=2) as out_pool,
+        tc.psum_pool(name="psum_once", bufs=1) as psum_once,
+        tc.psum_pool(name="psum_flip", bufs=4) as psum_flip,
     ):
         offsets = held.tile([P, N // 16], U16, name="offsets")
         nc.sync.dma_start(offsets[:], offs)
-
-        th_all = held.tile([P, KN], F32, name="th_all")
-        ineq_all = held.tile([P, KN], F32, name="ineq_all")
-        esign_all = held.tile([P, KN], F32, name="esign_all")
-        mask_all = held.tile([P, KN], F32, name="mask_all")
-        tau_all = held.tile([P, KQ], F32, name="tau_all")
-        nc.scalar.dma_start(th_all[:], th.rearrange("k n -> (k n)").partition_broadcast(P))
-        nc.gpsimd.dma_start(ineq_all[:], ineq.rearrange("k n -> (k n)").partition_broadcast(P))
-        nc.scalar.dma_start(esign_all[:], esign.rearrange("k n -> (k n)").partition_broadcast(P))
-        nc.gpsimd.dma_start(mask_all[:], mask.rearrange("k n -> (k n)").partition_broadcast(P))
-        nc.gpsimd.dma_start(tau_all[:], tau.rearrange("k q -> (k q)").partition_broadcast(P))
-
         x_blocks = []
         for b in range(BLOCKS):
             x_block = held.tile([P, S], F32, name=f"x_block{b}")
-            nc.sync.dma_start(x_block[:], x[b * P : (b + 1) * P, :])
+            nc.sync.dma_start(x_block[:], x_view[:, b, :])
             x_blocks.append(x_block)
+
+        th_all = held.tile([P, KN], F32, name="th_all")
+        nc.scalar.dma_start(th_all[:], th.rearrange("k n -> (k n)").partition_broadcast(P))
+        rows = held.tile([P, P], F32, name="rows")
+        nc.vector.memset(rows[:], 0.0)
+        nc.scalar.dma_start(rows[0:K, :], ineq)
+        nc.scalar.dma_start(rows[K : 2 * K, :], esign)
+        nc.scalar.dma_start(rows[2 * K : 3 * K, :], mask)
+        tau_row = held.tile([1, KQ], F32, name="tau_row")
+        nc.scalar.dma_start(tau_row[:], tau.rearrange("(o k) q -> o (k q)", o=1))
+
+        minus_ones = held.tile([1, P], F32, name="minus_ones")
+        nc.vector.memset(minus_ones[:], -1.0)
+        identity = held.tile([P, P], F32, name="identity")
+        make_identity(nc, identity[:])
+        in_group = held.tile([P, Q], F32, name="in_group")
+        nc.gpsimd.memset(in_group[:], 1.0)
+        nc.gpsimd.affine_select(
+            out=in_group[:], in_=in_group[:], pattern=[[-L, Q]], compare_op=IS_GE, fill=0.0, base=0, channel_multiplier=1
+        )
+        nc.gpsimd.affine_select(
+            out=in_group[:], in_=in_group[:], pattern=[[L, Q]], compare_op=IS_GE, fill=0.0, base=L - 1, channel_multiplier=-1
+        )
 
         nth = held.tile([P, KN], F32, name="nth")
         nc.vector.tensor_scalar_mul(nth[:], th_all[:], -1.0)
-        slope = held.tile([P, KN], F32, name="slope")
-        nc.scalar.activation(slope[:], ineq_all[:], FUNC.Tanh)
-        sign = held.tile([P, KN], F32, name="sign")
-        nc.scalar.activation(sign[:], esign_all[:], FUNC.Tanh)
-        gate = held.tile([P, KN], F32, name="gate")
-        nc.scalar.activation(gate[:], mask_all[:], FUNC.Sigmoid)
-        a = held.tile([P, KN], F32, name="a")
-        nc.gpsimd.tensor_tensor(a[:], gate[:], sign[:], MULT)
+        columns = psum_once.tile([P, P], F32, name="columns")
+        nc.tensor.transpose(columns[:], rows[:], identity[:])
+        tanhs = held.tile([P, 2 * K], F32, name="tanhs")
+        nc.scalar.activation(tanhs[:], columns[:, 0 : 2 * K], FUNC.Tanh)
+        steep = held.tile([P, K], F32, name="steep")
+        nc.scalar.mul(steep[:], tanhs[:, 0:K], 3.0)
+        gate = held.tile([P, K], F32, name="gate")
+        nc.scalar.activation(gate[:], columns[:, 2 * K : 3 * K], FUNC.Sigmoid)
+        a = held.tile([P, K], F32, name="a")
+        nc.vector.tensor_tensor(a[:], gate[:], tanhs[:, K : 2 * K], MULT)
+        weights = held.tile([P, KQ], SUM_DT, name="weights")
+        nc.vector.tensor_tensor(
+            weights[:].rearrange("p (k q) -> p k q", q=Q),
+            a[:].unsqueeze(2).to_broadcast([P, K, Q]),
+            in_group[:].unsqueeze(1).to_broadcast([P, K, Q]),
+            MULT,
+        )
 
-        for b in range(BLOCKS):
-            d = work.tile([P, KN], F32, name="d")
-            for k in range(K):
-                regime = slice(k * N, (k + 1) * N)
-                nc.vector.tensor_tensor(d[:, regime], x_blocks[b][:].indirect(offsets[:]), nth[:, regime], ADD)
-            steep = work.tile([P, KN], F32, name="steep")
-            nc.gpsimd.tensor_tensor(steep[:], d[:], slope[:], MULT)
-            rule = work.tile([P, KN], F32, name="rule")
-            nc.scalar.activation(rule[:], steep[:], FUNC.Tanh, scale=3.0)
-            evidence = work.tile([P, KN], F32, name="evidence")
-            nc.gpsimd.tensor_tensor(evidence[:], rule[:], a[:], MULT)
-            eg = work.tile([P, KQ], F32, name="eg")
-            nc.vector.tensor_reduce(
-                eg[:], evidence[:].rearrange("p (g l) -> p g l", l=L), axis=mybir.AxisListType.X, op=ADD
+        margins = []
+        for team in range(TEAMS):
+            margin = psum_once.tile([P, TEAM * KQ], F32, name=f"margin{team}")
+            nc.tensor.matmul(
+                margin[:].rearrange("p (i f) -> p i f", f=KQ),
+                lhsT=minus_ones[:],
+                rhs=tau_row[:].unsqueeze(1).to_broadcast([1, TEAM, KQ]),
+                start=True,
+                stop=False,
             )
-            margin = work.tile([P, KQ], F32, name="margin")
-            nc.vector.tensor_tensor(margin[:], eg[:], tau_all[:], SUBTRACT)
-            active = work.tile([P, KQ], F32, name="active")
-            nc.scalar.activation(active[:], margin[:], FUNC.Sigmoid, scale=6.0)
-            nc.sync.dma_start(out[b * P : (b + 1) * P, :], active[:])
+            margins.append(margin)
+
+        def compare(step):
+            team, k = divmod(step, K)
+            rules = []
+            for i in range(TEAM):
+                d = d_pool.tile([P, N], F32, name="d")
+                nc.vector.tensor_tensor(
+                    d[:], x_blocks[team * TEAM + i][:].indirect(offsets[:]), nth[:, k * N : (k + 1) * N], ADD
+                )
+                flipped = psum_flip.tile([P, P], F32, name="flipped")
+                nc.tensor.transpose(flipped[:], d[:], identity[:])
+                rule = rule_pool.tile([P, P], SUM_DT, name="rule")
+                nc.scalar.activation(rule[:], flipped[:], FUNC.Tanh, scale=steep[:, k : k + 1])
+                rules.append(rule)
+            return rules
+
+        def weigh(step, rules):
+            team, k = divmod(step, K)
+            margin = margins[team]
+            for i in range(TEAM):
+                nc.tensor.matmul(
+                    margin[:, i * KQ + k * Q : i * KQ + (k + 1) * Q],
+                    lhsT=rules[i][:],
+                    rhs=weights[:, k * Q : (k + 1) * Q],
+                    start=False,
+                    stop=(k == K - 1 and i == TEAM - 1),
+                )
+            if k == K - 1:
+                active = out_pool.tile([P, TEAM * KQ], F32, name="active")
+                nc.scalar.activation(active[:], margin[:], FUNC.Sigmoid, scale=6.0)
+                nc.sync.dma_start(
+                    out_view[:, team * TEAM : (team + 1) * TEAM, :], active[:].rearrange("p (i f) -> p i f", f=KQ)
+                )
+
+        rules_before = compare(0)
+        for step in range(1, STEPS):
+            rules = compare(step)
+            weigh(step - 1, rules_before)
+            rules_before = rules
+        weigh(STEPS - 1, rules_before)

@@ -2,7 +2,6 @@ import concourse.mybir as mybir
 from concourse.masks import make_identity
 
 F32 = mybir.dt.float32
-BF16 = mybir.dt.bfloat16
 U16 = mybir.dt.uint16
 ADD = mybir.AluOpType.add
 MULT = mybir.AluOpType.mult
@@ -17,7 +16,7 @@ BLOCKS = C // P
 TEAM = 4
 TEAMS = BLOCKS // TEAM
 STEPS = TEAMS * K
-SUM_DT = BF16
+SUM_DT = F32
 FLOPS = 2 * C * K * N
 
 

@@ -2,21 +2,18 @@ import concourse.mybir as mybir
 from concourse.masks import make_identity
 
 F32 = mybir.dt.float32
+BF16 = mybir.dt.bfloat16
 U16 = mybir.dt.uint16
 ADD = mybir.AluOpType.add
-MULT = mybir.AluOpType.mult
 IS_GE = mybir.AluOpType.is_ge
 FUNC = mybir.ActivationFunctionType
 
 P = 128
 C, S, K, Q, L, N = 1024, 256, 6, 16, 8, 128
-KN = K * N
 KQ = K * Q
 BLOCKS = C // P
 TEAM = 4
-TEAMS = BLOCKS // TEAM
-STEPS = TEAMS * K
-SUM_DT = F32
+STEPS = (BLOCKS // TEAM) * K
 FLOPS = 2 * C * K * N
 
 
@@ -26,22 +23,31 @@ def tile_regimerulesnet_kernel(tc, x, th, ineq, esign, mask, tau, offs, out):
     out_view = out.rearrange("(p b) f -> p b f", b=BLOCKS)
     with (
         tc.tile_pool(name="held", bufs=1) as held,
-        tc.tile_pool(name="d_pool", bufs=3 * TEAM) as d_pool,
+        tc.tile_pool(name="d_pool", bufs=16) as d_pool,
         tc.tile_pool(name="rule_pool", bufs=3 * TEAM) as rule_pool,
         tc.tile_pool(name="out_pool", bufs=2) as out_pool,
         tc.psum_pool(name="psum_once", bufs=1) as psum_once,
-        tc.psum_pool(name="psum_flip", bufs=4) as psum_flip,
+        tc.psum_pool(name="psum_flip", bufs=5) as psum_flip,
+        tc.psum_pool(name="psum_margin", bufs=2) as psum_margin,
     ):
         offsets = held.tile([P, N // 16], U16, name="offsets")
         nc.sync.dma_start(offsets[:], offs)
-        x_blocks = []
-        for b in range(BLOCKS):
+
+        def load_th(k):
+            th_all = held.tile([P, N], F32, name=f"th_all{k}")
+            nc.sync.dma_start(th_all[:], th[k, :].partition_broadcast(P))
+            return th_all
+
+        def load_x(b):
             x_block = held.tile([P, S], F32, name=f"x_block{b}")
             nc.sync.dma_start(x_block[:], x_view[:, b, :])
-            x_blocks.append(x_block)
+            return x_block
 
-        th_all = held.tile([P, KN], F32, name="th_all")
-        nc.scalar.dma_start(th_all[:], th.rearrange("k n -> (k n)").partition_broadcast(P))
+        th_alls = [load_th(0)]
+        x_blocks = [load_x(b) for b in range(TEAM)]
+        th_alls += [load_th(k) for k in range(1, K)]
+        x_blocks += [load_x(b) for b in range(TEAM, BLOCKS)]
+
         rows = held.tile([P, P], F32, name="rows")
         nc.vector.memset(rows[:], 0.0)
         nc.scalar.dma_start(rows[0:K, :], ineq)
@@ -63,29 +69,43 @@ def tile_regimerulesnet_kernel(tc, x, th, ineq, esign, mask, tau, offs, out):
             out=in_group[:], in_=in_group[:], pattern=[[L, Q]], compare_op=IS_GE, fill=0.0, base=L - 1, channel_multiplier=-1
         )
 
-        nth = held.tile([P, KN], F32, name="nth")
-        nc.vector.tensor_scalar_mul(nth[:], th_all[:], -1.0)
+        nths = []
+        for k in range(K):
+            nth = held.tile([P, N], F32, name=f"nth{k}")
+            nc.vector.tensor_scalar_mul(nth[:], th_alls[k][:], -1.0)
+            nths.append(nth)
         columns = psum_once.tile([P, P], F32, name="columns")
         nc.tensor.transpose(columns[:], rows[:], identity[:])
         tanhs = held.tile([P, 2 * K], F32, name="tanhs")
         nc.scalar.activation(tanhs[:], columns[:, 0 : 2 * K], FUNC.Tanh)
         steep = held.tile([P, K], F32, name="steep")
         nc.scalar.mul(steep[:], tanhs[:, 0:K], 3.0)
-        gate = held.tile([P, K], F32, name="gate")
-        nc.scalar.activation(gate[:], columns[:, 2 * K : 3 * K], FUNC.Sigmoid)
-        a = held.tile([P, K], F32, name="a")
-        nc.vector.tensor_tensor(a[:], gate[:], tanhs[:, K : 2 * K], MULT)
-        weights = held.tile([P, KQ], SUM_DT, name="weights")
-        nc.vector.tensor_tensor(
-            weights[:].rearrange("p (k q) -> p k q", q=Q),
-            a[:].unsqueeze(2).to_broadcast([P, K, Q]),
-            in_group[:].unsqueeze(1).to_broadcast([P, K, Q]),
-            MULT,
-        )
 
-        margins = []
-        for team in range(TEAMS):
-            margin = psum_once.tile([P, TEAM * KQ], F32, name=f"margin{team}")
+        def compare(step):
+            team, k = divmod(step, K)
+            rules = []
+            for i in range(TEAM):
+                d = d_pool.tile([P, N], F32, name="d")
+                nc.vector.tensor_tensor(d[:], x_blocks[team * TEAM + i][:].indirect(offsets[:]), nths[k][:], ADD)
+                flipped = psum_flip.tile([P, P], F32, name="flipped")
+                nc.tensor.transpose(flipped[:], d[:], identity[:])
+                rule = rule_pool.tile([P, P], BF16, name="rule")
+                nc.scalar.activation(rule[:], flipped[:], FUNC.Tanh, scale=steep[:, k : k + 1])
+                rules.append(rule)
+            return rules
+
+        def make_weights():
+            gate = held.tile([P, K], F32, name="gate")
+            nc.scalar.activation(gate[:], columns[:, 2 * K : 3 * K], FUNC.Sigmoid)
+            a = held.tile([P, K], F32, name="a")
+            weights = held.tile([P, KQ], BF16, name="weights")
+            for k in range(K):
+                nc.scalar.activation(a[:, k : k + 1], gate[:, k : k + 1], FUNC.Identity, scale=tanhs[:, K + k : K + k + 1])
+                nc.scalar.activation(weights[:, k * Q : (k + 1) * Q], in_group[:], FUNC.Identity, scale=a[:, k : k + 1])
+            return weights
+
+        def open_margin():
+            margin = psum_margin.tile([P, TEAM * KQ], F32, name="margin")
             nc.tensor.matmul(
                 margin[:].rearrange("p (i f) -> p i f", f=KQ),
                 lhsT=minus_ones[:],
@@ -93,26 +113,10 @@ def tile_regimerulesnet_kernel(tc, x, th, ineq, esign, mask, tau, offs, out):
                 start=True,
                 stop=False,
             )
-            margins.append(margin)
+            return margin
 
-        def compare(step):
-            team, k = divmod(step, K)
-            rules = []
-            for i in range(TEAM):
-                d = d_pool.tile([P, N], F32, name="d")
-                nc.vector.tensor_tensor(
-                    d[:], x_blocks[team * TEAM + i][:].indirect(offsets[:]), nth[:, k * N : (k + 1) * N], ADD
-                )
-                flipped = psum_flip.tile([P, P], F32, name="flipped")
-                nc.tensor.transpose(flipped[:], d[:], identity[:])
-                rule = rule_pool.tile([P, P], SUM_DT, name="rule")
-                nc.scalar.activation(rule[:], flipped[:], FUNC.Tanh, scale=steep[:, k : k + 1])
-                rules.append(rule)
-            return rules
-
-        def weigh(step, rules):
-            team, k = divmod(step, K)
-            margin = margins[team]
+        def weigh(step, rules, margin):
+            k = step % K
             for i in range(TEAM):
                 nc.tensor.matmul(
                     margin[:, i * KQ + k * Q : i * KQ + (k + 1) * Q],
@@ -121,16 +125,21 @@ def tile_regimerulesnet_kernel(tc, x, th, ineq, esign, mask, tau, offs, out):
                     start=False,
                     stop=(k == K - 1 and i == TEAM - 1),
                 )
-            if k == K - 1:
-                active = out_pool.tile([P, TEAM * KQ], F32, name="active")
-                nc.scalar.activation(active[:], margin[:], FUNC.Sigmoid, scale=6.0)
-                nc.sync.dma_start(
-                    out_view[:, team * TEAM : (team + 1) * TEAM, :], active[:].rearrange("p (i f) -> p i f", f=KQ)
-                )
 
-        rules_before = compare(0)
-        for step in range(1, STEPS):
-            rules = compare(step)
-            weigh(step - 1, rules_before)
-            rules_before = rules
-        weigh(STEPS - 1, rules_before)
+        def finish(team, margin):
+            active = out_pool.tile([P, TEAM * KQ], F32, name="active")
+            nc.scalar.activation(active[:], margin[:], FUNC.Sigmoid, scale=6.0)
+            nc.sync.dma_start(
+                out_view[:, team * TEAM : (team + 1) * TEAM, :], active[:].rearrange("p (i f) -> p i f", f=KQ)
+            )
+
+        rules_of = {0: compare(0)}
+        weights = make_weights()
+        for step in range(STEPS):
+            if step + 1 < STEPS:
+                rules_of[step + 1] = compare(step + 1)
+            if step % K == 0:
+                margin = open_margin()
+            weigh(step, rules_of[step], margin)
+            if step % K == K - 1:
+                finish(step // K, margin)

@@ -5,6 +5,7 @@ F32 = mybir.dt.float32
 BF16 = mybir.dt.bfloat16
 U16 = mybir.dt.uint16
 ADD = mybir.AluOpType.add
+SUBTRACT = mybir.AluOpType.subtract
 IS_GE = mybir.AluOpType.is_ge
 FUNC = mybir.ActivationFunctionType
 
@@ -28,7 +29,7 @@ def tile_regimerulesnet_kernel(tc, x, th, ineq, esign, mask, tau, offs, out):
         tc.tile_pool(name="out_pool", bufs=2) as out_pool,
         tc.psum_pool(name="psum_once", bufs=1) as psum_once,
         tc.psum_pool(name="psum_flip", bufs=5) as psum_flip,
-        tc.psum_pool(name="psum_margin", bufs=2) as psum_margin,
+        tc.psum_pool(name="psum_eg", bufs=2) as psum_eg,
     ):
         offsets = held.tile([P, N // 16], U16, name="offsets")
         nc.sync.dma_start(offsets[:], offs)
@@ -53,11 +54,9 @@ def tile_regimerulesnet_kernel(tc, x, th, ineq, esign, mask, tau, offs, out):
         nc.scalar.dma_start(rows[0:K, :], ineq)
         nc.scalar.dma_start(rows[K : 2 * K, :], esign)
         nc.scalar.dma_start(rows[2 * K : 3 * K, :], mask)
-        tau_row = held.tile([1, KQ], F32, name="tau_row")
-        nc.scalar.dma_start(tau_row[:], tau.rearrange("(o k) q -> o (k q)", o=1))
+        tau_all = held.tile([P, KQ], F32, name="tau_all")
+        nc.scalar.dma_start(tau_all[:], tau.rearrange("k q -> (k q)").partition_broadcast(P))
 
-        minus_ones = held.tile([1, P], F32, name="minus_ones")
-        nc.vector.memset(minus_ones[:], -1.0)
         identity = held.tile([P, P], F32, name="identity")
         make_identity(nc, identity[:])
         in_group = held.tile([P, Q], F32, name="in_group")
@@ -104,29 +103,25 @@ def tile_regimerulesnet_kernel(tc, x, th, ineq, esign, mask, tau, offs, out):
                 nc.scalar.activation(weights[:, k * Q : (k + 1) * Q], in_group[:], FUNC.Identity, scale=a[:, k : k + 1])
             return weights
 
-        def open_margin():
-            margin = psum_margin.tile([P, TEAM * KQ], F32, name="margin")
-            nc.tensor.matmul(
-                margin[:].rearrange("p (i f) -> p i f", f=KQ),
-                lhsT=minus_ones[:],
-                rhs=tau_row[:].unsqueeze(1).to_broadcast([1, TEAM, KQ]),
-                start=True,
-                stop=False,
-            )
-            return margin
-
-        def weigh(step, rules, margin):
+        def weigh(step, rules, eg):
             k = step % K
             for i in range(TEAM):
                 nc.tensor.matmul(
-                    margin[:, i * KQ + k * Q : i * KQ + (k + 1) * Q],
+                    eg[:, i * KQ + k * Q : i * KQ + (k + 1) * Q],
                     lhsT=rules[i][:],
                     rhs=weights[:, k * Q : (k + 1) * Q],
-                    start=False,
-                    stop=(k == K - 1 and i == TEAM - 1),
+                    start=True,
+                    stop=True,
                 )
 
-        def finish(team, margin):
+        def finish(team, eg):
+            margin = out_pool.tile([P, TEAM * KQ], F32, name="margin")
+            nc.vector.tensor_tensor(
+                margin[:].rearrange("p (i f) -> p i f", f=KQ),
+                eg[:].rearrange("p (i f) -> p i f", f=KQ),
+                tau_all[:].unsqueeze(1).to_broadcast([P, TEAM, KQ]),
+                SUBTRACT,
+            )
             active = out_pool.tile([P, TEAM * KQ], F32, name="active")
             nc.scalar.activation(active[:], margin[:], FUNC.Sigmoid, scale=6.0)
             nc.sync.dma_start(
@@ -139,7 +134,7 @@ def tile_regimerulesnet_kernel(tc, x, th, ineq, esign, mask, tau, offs, out):
             if step + 1 < STEPS:
                 rules_of[step + 1] = compare(step + 1)
             if step % K == 0:
-                margin = open_margin()
-            weigh(step, rules_of[step], margin)
+                eg = psum_eg.tile([P, TEAM * KQ], F32, name="eg")
+            weigh(step, rules_of[step], eg)
             if step % K == K - 1:
-                finish(step // K, margin)
+                finish(step // K, eg)

@@ -5,58 +5,50 @@ F32 = mybir.dt.float32
 BF16 = mybir.dt.bfloat16
 U16 = mybir.dt.uint16
 ADD = mybir.AluOpType.add
-SUBTRACT = mybir.AluOpType.subtract
 IS_GE = mybir.AluOpType.is_ge
 FUNC = mybir.ActivationFunctionType
 
 P = 128
 C, S, K, Q, L, N = 1024, 256, 6, 16, 8, 128
+KN = K * N
 KQ = K * Q
 BLOCKS = C // P
-TEAM = 4
-STEPS = (BLOCKS // TEAM) * K
+UNITS = BLOCKS * K
+LAG = 4
 FLOPS = 2 * C * K * N
 
 
 def tile_regimerulesnet_kernel(tc, x, th, ineq, esign, mask, tau, offs, out):
     nc = tc.nc
-    x_view = x.rearrange("(p b) s -> p b s", b=BLOCKS)
-    out_view = out.rearrange("(p b) f -> p b f", b=BLOCKS)
     with (
         tc.tile_pool(name="held", bufs=1) as held,
         tc.tile_pool(name="d_pool", bufs=16) as d_pool,
-        tc.tile_pool(name="rule_pool", bufs=3 * TEAM) as rule_pool,
+        tc.tile_pool(name="rule_pool", bufs=LAG + 4) as rule_pool,
         tc.tile_pool(name="out_pool", bufs=2) as out_pool,
         tc.psum_pool(name="psum_once", bufs=1) as psum_once,
         tc.psum_pool(name="psum_flip", bufs=5) as psum_flip,
-        tc.psum_pool(name="psum_eg", bufs=2) as psum_eg,
+        tc.psum_pool(name="psum_margin", bufs=2) as psum_margin,
     ):
         offsets = held.tile([P, N // 16], U16, name="offsets")
         nc.sync.dma_start(offsets[:], offs)
-
-        def load_th(k):
-            th_all = held.tile([P, N], F32, name=f"th_all{k}")
-            nc.sync.dma_start(th_all[:], th[k, :].partition_broadcast(P))
-            return th_all
-
-        def load_x(b):
+        x_blocks = []
+        for b in range(BLOCKS):
             x_block = held.tile([P, S], F32, name=f"x_block{b}")
-            nc.sync.dma_start(x_block[:], x_view[:, b, :])
-            return x_block
+            nc.sync.dma_start(x_block[:], x[b * P : (b + 1) * P, :])
+            x_blocks.append(x_block)
 
-        th_alls = [load_th(0)]
-        x_blocks = [load_x(b) for b in range(TEAM)]
-        th_alls += [load_th(k) for k in range(1, K)]
-        x_blocks += [load_x(b) for b in range(TEAM, BLOCKS)]
-
+        th_all = held.tile([P, KN], F32, name="th_all")
+        nc.scalar.dma_start(th_all[:], th.rearrange("k n -> (k n)").partition_broadcast(P))
         rows = held.tile([P, P], F32, name="rows")
         nc.vector.memset(rows[:], 0.0)
         nc.scalar.dma_start(rows[0:K, :], ineq)
         nc.scalar.dma_start(rows[K : 2 * K, :], esign)
         nc.scalar.dma_start(rows[2 * K : 3 * K, :], mask)
-        tau_all = held.tile([P, KQ], F32, name="tau_all")
-        nc.scalar.dma_start(tau_all[:], tau.rearrange("k q -> (k q)").partition_broadcast(P))
+        tau_row = held.tile([1, KQ], F32, name="tau_row")
+        nc.scalar.dma_start(tau_row[:], tau.rearrange("(o k) q -> o (k q)", o=1))
 
+        minus_ones = held.tile([1, P], F32, name="minus_ones")
+        nc.vector.memset(minus_ones[:], -1.0)
         identity = held.tile([P, P], F32, name="identity")
         make_identity(nc, identity[:])
         in_group = held.tile([P, Q], F32, name="in_group")
@@ -68,11 +60,8 @@ def tile_regimerulesnet_kernel(tc, x, th, ineq, esign, mask, tau, offs, out):
             out=in_group[:], in_=in_group[:], pattern=[[L, Q]], compare_op=IS_GE, fill=0.0, base=L - 1, channel_multiplier=-1
         )
 
-        nths = []
-        for k in range(K):
-            nth = held.tile([P, N], F32, name=f"nth{k}")
-            nc.vector.tensor_scalar_mul(nth[:], th_alls[k][:], -1.0)
-            nths.append(nth)
+        nth = held.tile([P, KN], F32, name="nth")
+        nc.vector.tensor_scalar_mul(nth[:], th_all[:], -1.0)
         columns = psum_once.tile([P, P], F32, name="columns")
         nc.tensor.transpose(columns[:], rows[:], identity[:])
         tanhs = held.tile([P, 2 * K], F32, name="tanhs")
@@ -80,18 +69,15 @@ def tile_regimerulesnet_kernel(tc, x, th, ineq, esign, mask, tau, offs, out):
         steep = held.tile([P, K], F32, name="steep")
         nc.scalar.mul(steep[:], tanhs[:, 0:K], 3.0)
 
-        def compare(step):
-            team, k = divmod(step, K)
-            rules = []
-            for i in range(TEAM):
-                d = d_pool.tile([P, N], F32, name="d")
-                nc.vector.tensor_tensor(d[:], x_blocks[team * TEAM + i][:].indirect(offsets[:]), nths[k][:], ADD)
-                flipped = psum_flip.tile([P, P], F32, name="flipped")
-                nc.tensor.transpose(flipped[:], d[:], identity[:])
-                rule = rule_pool.tile([P, P], BF16, name="rule")
-                nc.scalar.activation(rule[:], flipped[:], FUNC.Tanh, scale=steep[:, k : k + 1])
-                rules.append(rule)
-            return rules
+        def compare(unit):
+            b, k = divmod(unit, K)
+            d = d_pool.tile([P, N], F32, name="d")
+            nc.vector.tensor_tensor(d[:], x_blocks[b][:].indirect(offsets[:]), nth[:, k * N : (k + 1) * N], ADD)
+            flipped = psum_flip.tile([P, P], F32, name="flipped")
+            nc.tensor.transpose(flipped[:], d[:], identity[:])
+            rule = rule_pool.tile([P, P], BF16, name="rule")
+            nc.scalar.activation(rule[:], flipped[:], FUNC.Tanh, scale=steep[:, k : k + 1])
+            return rule
 
         def make_weights():
             gate = held.tile([P, K], F32, name="gate")
@@ -103,38 +89,30 @@ def tile_regimerulesnet_kernel(tc, x, th, ineq, esign, mask, tau, offs, out):
                 nc.scalar.activation(weights[:, k * Q : (k + 1) * Q], in_group[:], FUNC.Identity, scale=a[:, k : k + 1])
             return weights
 
-        def weigh(step, rules, eg):
-            k = step % K
-            for i in range(TEAM):
-                nc.tensor.matmul(
-                    eg[:, i * KQ + k * Q : i * KQ + (k + 1) * Q],
-                    lhsT=rules[i][:],
-                    rhs=weights[:, k * Q : (k + 1) * Q],
-                    start=True,
-                    stop=True,
-                )
+        def open_margin():
+            margin = psum_margin.tile([P, KQ], F32, name="margin")
+            nc.tensor.matmul(margin[:], lhsT=minus_ones[:], rhs=tau_row[:], start=True, stop=False)
+            return margin
 
-        def finish(team, eg):
-            margin = out_pool.tile([P, TEAM * KQ], F32, name="margin")
-            nc.vector.tensor_tensor(
-                margin[:].rearrange("p (i f) -> p i f", f=KQ),
-                eg[:].rearrange("p (i f) -> p i f", f=KQ),
-                tau_all[:].unsqueeze(1).to_broadcast([P, TEAM, KQ]),
-                SUBTRACT,
-            )
-            active = out_pool.tile([P, TEAM * KQ], F32, name="active")
+        def finish(b, margin):
+            active = out_pool.tile([P, KQ], F32, name="active")
             nc.scalar.activation(active[:], margin[:], FUNC.Sigmoid, scale=6.0)
-            nc.sync.dma_start(
-                out_view[:, team * TEAM : (team + 1) * TEAM, :], active[:].rearrange("p (i f) -> p i f", f=KQ)
-            )
+            nc.sync.dma_start(out[b * P : (b + 1) * P, :], active[:])
 
-        rules_of = {0: compare(0)}
+        rules = [compare(unit) for unit in range(LAG)]
         weights = make_weights()
-        for step in range(STEPS):
-            if step + 1 < STEPS:
-                rules_of[step + 1] = compare(step + 1)
-            if step % K == 0:
-                eg = psum_eg.tile([P, TEAM * KQ], F32, name="eg")
-            weigh(step, rules_of[step], eg)
-            if step % K == K - 1:
-                finish(step // K, eg)
+        for unit in range(UNITS):
+            if unit + LAG < UNITS:
+                rules.append(compare(unit + LAG))
+            b, k = divmod(unit, K)
+            if k == 0:
+                margin = open_margin()
+            nc.tensor.matmul(
+                margin[:, k * Q : (k + 1) * Q],
+                lhsT=rules[unit][:],
+                rhs=weights[:, k * Q : (k + 1) * Q],
+                start=False,
+                stop=(k == K - 1),
+            )
+            if k == K - 1:
+                finish(b, margin)

@@ -5,50 +5,58 @@ F32 = mybir.dt.float32
 BF16 = mybir.dt.bfloat16
 U16 = mybir.dt.uint16
 ADD = mybir.AluOpType.add
+SUBTRACT = mybir.AluOpType.subtract
 IS_GE = mybir.AluOpType.is_ge
 FUNC = mybir.ActivationFunctionType
 
 P = 128
 C, S, K, Q, L, N = 1024, 256, 6, 16, 8, 128
-KN = K * N
 KQ = K * Q
 BLOCKS = C // P
-UNITS = BLOCKS * K
-LAG = 4
+TEAM = 4
+STEPS = (BLOCKS // TEAM) * K
 FLOPS = 2 * C * K * N
 
 
 def tile_regimerulesnet_kernel(tc, x, th, ineq, esign, mask, tau, offs, out):
     nc = tc.nc
+    x_view = x.rearrange("(p b) s -> p b s", b=BLOCKS)
+    out_view = out.rearrange("(p b) f -> p b f", b=BLOCKS)
     with (
         tc.tile_pool(name="held", bufs=1) as held,
         tc.tile_pool(name="d_pool", bufs=16) as d_pool,
-        tc.tile_pool(name="rule_pool", bufs=LAG + 4) as rule_pool,
+        tc.tile_pool(name="rule_pool", bufs=3 * TEAM) as rule_pool,
         tc.tile_pool(name="out_pool", bufs=2) as out_pool,
         tc.psum_pool(name="psum_once", bufs=1) as psum_once,
         tc.psum_pool(name="psum_flip", bufs=5) as psum_flip,
-        tc.psum_pool(name="psum_margin", bufs=2) as psum_margin,
+        tc.psum_pool(name="psum_eg", bufs=2) as psum_eg,
     ):
         offsets = held.tile([P, N // 16], U16, name="offsets")
         nc.sync.dma_start(offsets[:], offs)
-        x_blocks = []
-        for b in range(BLOCKS):
-            x_block = held.tile([P, S], F32, name=f"x_block{b}")
-            nc.sync.dma_start(x_block[:], x[b * P : (b + 1) * P, :])
-            x_blocks.append(x_block)
 
-        th_all = held.tile([P, KN], F32, name="th_all")
-        nc.scalar.dma_start(th_all[:], th.rearrange("k n -> (k n)").partition_broadcast(P))
+        def load_th(k):
+            th_all = held.tile([P, N], F32, name=f"th_all{k}")
+            nc.sync.dma_start(th_all[:], th[k, :].partition_broadcast(P))
+            return th_all
+
+        def load_x(b):
+            x_block = held.tile([P, S], F32, name=f"x_block{b}")
+            nc.sync.dma_start(x_block[:], x_view[:, b, :])
+            return x_block
+
+        th_alls = [load_th(0)]
+        x_blocks = [load_x(b) for b in range(TEAM)]
+        th_alls += [load_th(k) for k in range(1, K)]
+        x_blocks += [load_x(b) for b in range(TEAM, BLOCKS)]
+
         rows = held.tile([P, P], F32, name="rows")
         nc.vector.memset(rows[:], 0.0)
         nc.scalar.dma_start(rows[0:K, :], ineq)
         nc.scalar.dma_start(rows[K : 2 * K, :], esign)
         nc.scalar.dma_start(rows[2 * K : 3 * K, :], mask)
-        tau_row = held.tile([1, KQ], F32, name="tau_row")
-        nc.scalar.dma_start(tau_row[:], tau.rearrange("(o k) q -> o (k q)", o=1))
+        tau_all = held.tile([P, KQ], F32, name="tau_all")
+        nc.scalar.dma_start(tau_all[:], tau.rearrange("k q -> (k q)").partition_broadcast(P))
 
-        minus_ones = held.tile([1, P], F32, name="minus_ones")
-        nc.vector.memset(minus_ones[:], -1.0)
         identity = held.tile([P, P], F32, name="identity")
         make_identity(nc, identity[:])
         in_group = held.tile([P, Q], F32, name="in_group")
@@ -60,8 +68,11 @@ def tile_regimerulesnet_kernel(tc, x, th, ineq, esign, mask, tau, offs, out):
             out=in_group[:], in_=in_group[:], pattern=[[L, Q]], compare_op=IS_GE, fill=0.0, base=L - 1, channel_multiplier=-1
         )
 
-        nth = held.tile([P, KN], F32, name="nth")
-        nc.vector.tensor_scalar_mul(nth[:], th_all[:], -1.0)
+        nths = []
+        for k in range(K):
+            nth = held.tile([P, N], F32, name=f"nth{k}")
+            nc.vector.tensor_scalar_mul(nth[:], th_alls[k][:], -1.0)
+            nths.append(nth)
         columns = psum_once.tile([P, P], F32, name="columns")
         nc.tensor.transpose(columns[:], rows[:], identity[:])
         tanhs = held.tile([P, 2 * K], F32, name="tanhs")
@@ -69,15 +80,18 @@ def tile_regimerulesnet_kernel(tc, x, th, ineq, esign, mask, tau, offs, out):
         steep = held.tile([P, K], F32, name="steep")
         nc.scalar.mul(steep[:], tanhs[:, 0:K], 3.0)
 
-        def compare(unit):
-            b, k = divmod(unit, K)
-            d = d_pool.tile([P, N], F32, name="d")
-            nc.vector.tensor_tensor(d[:], x_blocks[b][:].indirect(offsets[:]), nth[:, k * N : (k + 1) * N], ADD)
-            flipped = psum_flip.tile([P, P], F32, name="flipped")
-            nc.tensor.transpose(flipped[:], d[:], identity[:])
-            rule = rule_pool.tile([P, P], BF16, name="rule")
-            nc.scalar.activation(rule[:], flipped[:], FUNC.Tanh, scale=steep[:, k : k + 1])
-            return rule
+        def compare(step):
+            team, k = divmod(step, K)
+            rules = []
+            for i in range(TEAM):
+                d = d_pool.tile([P, N], F32, name="d")
+                nc.vector.tensor_tensor(d[:], x_blocks[team * TEAM + i][:].indirect(offsets[:]), nths[k][:], ADD)
+                flipped = psum_flip.tile([P, P], F32, name="flipped")
+                nc.tensor.transpose(flipped[:], d[:], identity[:])
+                rule = rule_pool.tile([P, P], BF16, name="rule")
+                nc.scalar.activation(rule[:], flipped[:], FUNC.Tanh, scale=steep[:, k : k + 1])
+                rules.append(rule)
+            return rules
 
         def make_weights():
             gate = held.tile([P, K], F32, name="gate")
@@ -89,30 +103,39 @@ def tile_regimerulesnet_kernel(tc, x, th, ineq, esign, mask, tau, offs, out):
                 nc.scalar.activation(weights[:, k * Q : (k + 1) * Q], in_group[:], FUNC.Identity, scale=a[:, k : k + 1])
             return weights
 
-        def open_margin():
-            margin = psum_margin.tile([P, KQ], F32, name="margin")
-            nc.tensor.matmul(margin[:], lhsT=minus_ones[:], rhs=tau_row[:], start=True, stop=False)
-            return margin
+        def weigh(step, rules, eg):
+            k = step % K
+            for i in range(TEAM):
+                nc.tensor.matmul(
+                    eg[:, i * KQ + k * Q : i * KQ + (k + 1) * Q],
+                    lhsT=rules[i][:],
+                    rhs=weights[:, k * Q : (k + 1) * Q],
+                    start=True,
+                    stop=True,
+                )
 
-        def finish(b, margin):
-            active = out_pool.tile([P, KQ], F32, name="active")
-            nc.scalar.activation(active[:], margin[:], FUNC.Sigmoid, scale=6.0)
-            nc.sync.dma_start(out[b * P : (b + 1) * P, :], active[:])
-
-        rules = [compare(unit) for unit in range(LAG)]
-        weights = make_weights()
-        for unit in range(UNITS):
-            if unit + LAG < UNITS:
-                rules.append(compare(unit + LAG))
-            b, k = divmod(unit, K)
-            if k == 0:
-                margin = open_margin()
-            nc.tensor.matmul(
-                margin[:, k * Q : (k + 1) * Q],
-                lhsT=rules[unit][:],
-                rhs=weights[:, k * Q : (k + 1) * Q],
-                start=False,
-                stop=(k == K - 1),
+        def finish(team, eg):
+            margin = out_pool.tile([P, TEAM * KQ], F32, name="margin")
+            nc.vector.tensor_tensor(
+                margin[:].rearrange("p (i f) -> p i f", f=KQ),
+                eg[:].rearrange("p (i f) -> p i f", f=KQ),
+                tau_all[:].unsqueeze(1).to_broadcast([P, TEAM, KQ]),
+                SUBTRACT,
             )
-            if k == K - 1:
-                finish(b, margin)
+            active = out_pool.tile([P, TEAM * KQ], F32, name="active")
+            nc.scalar.activation(active[:], margin[:], FUNC.Sigmoid, scale=6.0)
+            nc.sync.dma_start(
+                out_view[:, team * TEAM : (team + 1) * TEAM, :], active[:].rearrange("p (i f) -> p i f", f=KQ)
+            )
+
+        rules_of = {0: compare(0)}
+        weights = make_weights()
+        egs = []
+        for step in range(STEPS):
+            if step + 1 < STEPS:
+                rules_of[step + 1] = compare(step + 1)
+            if step % K == 0:
+                egs.append(psum_eg.tile([P, TEAM * KQ], F32, name="eg"))
+            weigh(step, rules_of[step], egs[-1])
+        for team, eg in enumerate(egs):
+            finish(team, eg)

@@ -11,6 +11,7 @@ FUNC = mybir.ActivationFunctionType
 
 P = 128
 C, S, K, Q, L, N = 1024, 256, 6, 16, 8, 128
+KN = K * N
 KQ = K * Q
 BLOCKS = C // P
 TEAM = 4
@@ -29,26 +30,18 @@ def tile_regimerulesnet_kernel(tc, x, th, ineq, esign, mask, tau, offs, out):
         tc.tile_pool(name="out_pool", bufs=2) as out_pool,
         tc.psum_pool(name="psum_once", bufs=1) as psum_once,
         tc.psum_pool(name="psum_flip", bufs=5) as psum_flip,
-        tc.psum_pool(name="psum_eg", bufs=2) as psum_eg,
+        tc.psum_pool(name="psum_margin", bufs=2) as psum_margin,
     ):
         offsets = held.tile([P, N // 16], U16, name="offsets")
         nc.sync.dma_start(offsets[:], offs)
-
-        def load_th(k):
-            th_all = held.tile([P, N], F32, name=f"th_all{k}")
-            nc.sync.dma_start(th_all[:], th[k, :].partition_broadcast(P))
-            return th_all
-
-        def load_x(b):
+        x_blocks = []
+        for b in range(BLOCKS):
             x_block = held.tile([P, S], F32, name=f"x_block{b}")
             nc.sync.dma_start(x_block[:], x_view[:, b, :])
-            return x_block
+            x_blocks.append(x_block)
 
-        th_alls = [load_th(0)]
-        x_blocks = [load_x(b) for b in range(TEAM)]
-        th_alls += [load_th(k) for k in range(1, K)]
-        x_blocks += [load_x(b) for b in range(TEAM, BLOCKS)]
-
+        th_all = held.tile([P, KN], F32, name="th_all")
+        nc.scalar.dma_start(th_all[:], th.rearrange("k n -> (k n)").partition_broadcast(P))
         rows = held.tile([P, P], F32, name="rows")
         nc.vector.memset(rows[:], 0.0)
         nc.scalar.dma_start(rows[0:K, :], ineq)
@@ -67,12 +60,11 @@ def tile_regimerulesnet_kernel(tc, x, th, ineq, esign, mask, tau, offs, out):
         nc.gpsimd.affine_select(
             out=in_group[:], in_=in_group[:], pattern=[[L, Q]], compare_op=IS_GE, fill=0.0, base=L - 1, channel_multiplier=-1
         )
+        minus_share = held.tile([P, P], BF16, name="minus_share")
+        nc.gpsimd.memset(minus_share[:], -1.0 / P)
 
-        nths = []
-        for k in range(K):
-            nth = held.tile([P, N], F32, name=f"nth{k}")
-            nc.vector.tensor_scalar_mul(nth[:], th_alls[k][:], -1.0)
-            nths.append(nth)
+        nth = held.tile([P, KN], F32, name="nth")
+        nc.vector.tensor_scalar_mul(nth[:], th_all[:], -1.0)
         columns = psum_once.tile([P, P], F32, name="columns")
         nc.tensor.transpose(columns[:], rows[:], identity[:])
         tanhs = held.tile([P, 2 * K], F32, name="tanhs")
@@ -85,7 +77,9 @@ def tile_regimerulesnet_kernel(tc, x, th, ineq, esign, mask, tau, offs, out):
             rules = []
             for i in range(TEAM):
                 d = d_pool.tile([P, N], F32, name="d")
-                nc.vector.tensor_tensor(d[:], x_blocks[team * TEAM + i][:].indirect(offsets[:]), nths[k][:], ADD)
+                nc.vector.tensor_tensor(
+                    d[:], x_blocks[team * TEAM + i][:].indirect(offsets[:]), nth[:, k * N : (k + 1) * N], ADD
+                )
                 flipped = psum_flip.tile([P, P], F32, name="flipped")
                 nc.tensor.transpose(flipped[:], d[:], identity[:])
                 rule = rule_pool.tile([P, P], BF16, name="rule")
@@ -103,25 +97,37 @@ def tile_regimerulesnet_kernel(tc, x, th, ineq, esign, mask, tau, offs, out):
                 nc.scalar.activation(weights[:, k * Q : (k + 1) * Q], in_group[:], FUNC.Identity, scale=a[:, k : k + 1])
             return weights
 
-        def weigh(step, rules, eg):
+        def split_tau():
+            tau_high = held.tile([P, KQ], BF16, name="tau_high")
+            nc.vector.tensor_copy(tau_high[:], tau_all[:])
+            tau_low = held.tile([P, KQ], BF16, name="tau_low")
+            nc.vector.tensor_tensor(tau_low[:], tau_all[:], tau_high[:], SUBTRACT)
+            return tau_high, tau_low
+
+        def open_margin():
+            margin = psum_margin.tile([P, TEAM * KQ], F32, name="margin")
+            for t, term in enumerate(tau_terms):
+                nc.tensor.matmul(
+                    margin[:].rearrange("p (i f) -> p i f", f=KQ),
+                    lhsT=minus_share[:],
+                    rhs=term[:].unsqueeze(1).to_broadcast([P, TEAM, KQ]),
+                    start=(t == 0),
+                    stop=False,
+                )
+            return margin
+
+        def weigh(step, rules, margin):
             k = step % K
             for i in range(TEAM):
                 nc.tensor.matmul(
-                    eg[:, i * KQ + k * Q : i * KQ + (k + 1) * Q],
+                    margin[:, i * KQ + k * Q : i * KQ + (k + 1) * Q],
                     lhsT=rules[i][:],
                     rhs=weights[:, k * Q : (k + 1) * Q],
-                    start=True,
-                    stop=True,
+                    start=False,
+                    stop=(k == K - 1 and i == TEAM - 1),
                 )
 
-        def finish(team, eg):
-            margin = out_pool.tile([P, TEAM * KQ], F32, name="margin")
-            nc.vector.tensor_tensor(
-                margin[:].rearrange("p (i f) -> p i f", f=KQ),
-                eg[:].rearrange("p (i f) -> p i f", f=KQ),
-                tau_all[:].unsqueeze(1).to_broadcast([P, TEAM, KQ]),
-                SUBTRACT,
-            )
+        def finish(team, margin):
             active = out_pool.tile([P, TEAM * KQ], F32, name="active")
             nc.scalar.activation(active[:], margin[:], FUNC.Sigmoid, scale=6.0)
             nc.sync.dma_start(
@@ -130,12 +136,12 @@ def tile_regimerulesnet_kernel(tc, x, th, ineq, esign, mask, tau, offs, out):
 
         rules_of = {0: compare(0)}
         weights = make_weights()
-        egs = []
+        tau_terms = split_tau()
         for step in range(STEPS):
             if step + 1 < STEPS:
                 rules_of[step + 1] = compare(step + 1)
             if step % K == 0:
-                egs.append(psum_eg.tile([P, TEAM * KQ], F32, name="eg"))
-            weigh(step, rules_of[step], egs[-1])
-        for team, eg in enumerate(egs):
-            finish(team, eg)
+                margin = open_margin()
+            weigh(step, rules_of[step], margin)
+            if step % K == K - 1:
+                finish(step // K, margin)

@@ -6,16 +6,16 @@ BF16 = mybir.dt.bfloat16
 U16 = mybir.dt.uint16
 ADD = mybir.AluOpType.add
 SUBTRACT = mybir.AluOpType.subtract
+MULT = mybir.AluOpType.mult
 IS_GE = mybir.AluOpType.is_ge
 FUNC = mybir.ActivationFunctionType
 
 P = 128
 C, S, K, Q, L, N = 1024, 256, 6, 16, 8, 128
-KN = K * N
 KQ = K * Q
 BLOCKS = C // P
 TEAM = 4
-STEPS = (BLOCKS // TEAM) * K
+TEAMS = BLOCKS // TEAM
 FLOPS = 2 * C * K * N
 
 
@@ -25,11 +25,11 @@ def tile_regimerulesnet_kernel(tc, x, th, ineq, esign, mask, tau, offs, out):
     out_view = out.rearrange("(p b) f -> p b f", b=BLOCKS)
     with (
         tc.tile_pool(name="held", bufs=1) as held,
-        tc.tile_pool(name="d_pool", bufs=16) as d_pool,
-        tc.tile_pool(name="rule_pool", bufs=3 * TEAM) as rule_pool,
+        tc.tile_pool(name="d_pool", bufs=BLOCKS) as d_pool,
+        tc.tile_pool(name="rule_pool", bufs=3) as rule_pool,
         tc.tile_pool(name="out_pool", bufs=2) as out_pool,
         tc.psum_pool(name="psum_once", bufs=1) as psum_once,
-        tc.psum_pool(name="psum_flip", bufs=5) as psum_flip,
+        tc.psum_pool(name="psum_flip", bufs=2) as psum_flip,
         tc.psum_pool(name="psum_margin", bufs=2) as psum_margin,
     ):
         offsets = held.tile([P, N // 16], U16, name="offsets")
@@ -40,13 +40,14 @@ def tile_regimerulesnet_kernel(tc, x, th, ineq, esign, mask, tau, offs, out):
             nc.sync.dma_start(x_block[:], x_view[:, b, :])
             x_blocks.append(x_block)
 
-        th_all = held.tile([P, KN], F32, name="th_all")
-        nc.scalar.dma_start(th_all[:], th.rearrange("k n -> (k n)").partition_broadcast(P))
+        th0_all = held.tile([P, N], F32, name="th0_all")
+        nc.scalar.dma_start(th0_all[:], th.rearrange("k n -> (k n)")[0:N].partition_broadcast(P))
         rows = held.tile([P, P], F32, name="rows")
         nc.vector.memset(rows[:], 0.0)
         nc.scalar.dma_start(rows[0:K, :], ineq)
         nc.scalar.dma_start(rows[K : 2 * K, :], esign)
         nc.scalar.dma_start(rows[2 * K : 3 * K, :], mask)
+        nc.scalar.dma_start(rows[3 * K : 4 * K, :], th)
         tau_all = held.tile([P, KQ], F32, name="tau_all")
         nc.scalar.dma_start(tau_all[:], tau.rearrange("k q -> (k q)").partition_broadcast(P))
 
@@ -63,39 +64,42 @@ def tile_regimerulesnet_kernel(tc, x, th, ineq, esign, mask, tau, offs, out):
         minus_share = held.tile([P, P], BF16, name="minus_share")
         nc.gpsimd.memset(minus_share[:], -1.0 / P)
 
-        nth = held.tile([P, KN], F32, name="nth")
-        nc.vector.tensor_scalar_mul(nth[:], th_all[:], -1.0)
-        columns = psum_once.tile([P, P], F32, name="columns")
-        nc.tensor.transpose(columns[:], rows[:], identity[:])
-        tanhs = held.tile([P, 2 * K], F32, name="tanhs")
-        nc.scalar.activation(tanhs[:], columns[:, 0 : 2 * K], FUNC.Tanh)
-        steep = held.tile([P, K], F32, name="steep")
-        nc.scalar.mul(steep[:], tanhs[:, 0:K], 3.0)
+        nth0 = held.tile([P, N], F32, name="nth0")
+        nc.vector.tensor_scalar_mul(nth0[:], th0_all[:], -1.0)
 
-        def compare(step):
-            team, k = divmod(step, K)
-            rules = []
+        def look_up(team):
+            flipped = psum_flip.tile([P, TEAM * P], F32, name="flipped")
             for i in range(TEAM):
-                d = d_pool.tile([P, N], F32, name="d")
-                nc.vector.tensor_tensor(
-                    d[:], x_blocks[team * TEAM + i][:].indirect(offsets[:]), nth[:, k * N : (k + 1) * N], ADD
-                )
-                flipped = psum_flip.tile([P, P], F32, name="flipped")
-                nc.tensor.transpose(flipped[:], d[:], identity[:])
-                rule = rule_pool.tile([P, P], BF16, name="rule")
-                nc.scalar.activation(rule[:], flipped[:], FUNC.Tanh, scale=steep[:, k : k + 1])
-                rules.append(rule)
-            return rules
+                d0 = d_pool.tile([P, N], F32, name="d0")
+                nc.vector.tensor_tensor(d0[:], x_blocks[team * TEAM + i][:].indirect(offsets[:]), nth0[:], ADD)
+                nc.tensor.transpose(flipped[:, i * P : (i + 1) * P], d0[:], identity[:])
+            return flipped
 
-        def make_weights():
+        def flip_parameters():
+            columns = psum_once.tile([P, P], F32, name="columns")
+            nc.tensor.transpose(columns[:], rows[:], identity[:])
             gate = held.tile([P, K], F32, name="gate")
             nc.scalar.activation(gate[:], columns[:, 2 * K : 3 * K], FUNC.Sigmoid)
+            tanhs = held.tile([P, 2 * K], F32, name="tanhs")
+            nc.scalar.activation(tanhs[:], columns[:, 0 : 2 * K], FUNC.Tanh)
+            th_columns = held.tile([P, K], F32, name="th_columns")
+            nc.vector.tensor_copy(th_columns[:], columns[:, 3 * K : 4 * K])
+            above = held.tile([P, K], F32, name="above")
+            nc.vector.tensor_scalar_sub(above[:], th_columns[:], th_columns[:, 0:1])
+            steep = held.tile([P, K], F32, name="steep")
+            nc.vector.tensor_scalar_mul(steep[:], tanhs[:, 0:K], 3.0)
+            shift = held.tile([P, K], F32, name="shift")
+            nc.vector.scalar_tensor_tensor(shift[:], above[:], -3.0, tanhs[:, 0:K], MULT, MULT)
             a = held.tile([P, K], F32, name="a")
+            nc.vector.tensor_tensor(a[:], gate[:], tanhs[:, K : 2 * K], MULT)
             weights = held.tile([P, KQ], BF16, name="weights")
-            for k in range(K):
-                nc.scalar.activation(a[:, k : k + 1], gate[:, k : k + 1], FUNC.Identity, scale=tanhs[:, K + k : K + k + 1])
-                nc.scalar.activation(weights[:, k * Q : (k + 1) * Q], in_group[:], FUNC.Identity, scale=a[:, k : k + 1])
-            return weights
+            nc.vector.tensor_tensor(
+                weights[:].rearrange("p (k q) -> p k q", q=Q),
+                in_group[:].unsqueeze(1).to_broadcast([P, K, Q]),
+                a[:].unsqueeze(2).to_broadcast([P, K, Q]),
+                MULT,
+            )
+            return steep, shift, weights
 
         def split_tau():
             tau_high = held.tile([P, KQ], BF16, name="tau_high")
@@ -116,12 +120,13 @@ def tile_regimerulesnet_kernel(tc, x, th, ineq, esign, mask, tau, offs, out):
                 )
             return margin
 
-        def weigh(step, rules, margin):
-            k = step % K
+        def compare_and_weigh(k, flipped, margin):
+            rule = rule_pool.tile([P, TEAM * P], BF16, name="rule")
+            nc.scalar.activation(rule[:], flipped[:], FUNC.Tanh, scale=steep[:, k : k + 1], bias=shift[:, k : k + 1])
             for i in range(TEAM):
                 nc.tensor.matmul(
                     margin[:, i * KQ + k * Q : i * KQ + (k + 1) * Q],
-                    lhsT=rules[i][:],
+                    lhsT=rule[:, i * P : (i + 1) * P],
                     rhs=weights[:, k * Q : (k + 1) * Q],
                     start=False,
                     stop=(k == K - 1 and i == TEAM - 1),
@@ -134,14 +139,16 @@ def tile_regimerulesnet_kernel(tc, x, th, ineq, esign, mask, tau, offs, out):
                 out_view[:, team * TEAM : (team + 1) * TEAM, :], active[:].rearrange("p (i f) -> p i f", f=KQ)
             )
 
-        rules_of = {0: compare(0)}
-        weights = make_weights()
+        flipped_of = {0: look_up(0)}
+        steep, shift, weights = flip_parameters()
         tau_terms = split_tau()
-        for step in range(STEPS):
-            if step + 1 < STEPS:
-                rules_of[step + 1] = compare(step + 1)
-            if step % K == 0:
-                margin = open_margin()
-            weigh(step, rules_of[step], margin)
-            if step % K == K - 1:
-                finish(step // K, margin)
+        margin_of = {}
+        for team in range(TEAMS):
+            if team + 1 < TEAMS:
+                flipped_of[team + 1] = look_up(team + 1)
+            margin_of[team] = open_margin()
+            for k in range(K):
+                compare_and_weigh(k, flipped_of[team], margin_of[team])
+                if k == 0 and team > 0:
+                    finish(team - 1, margin_of[team - 1])
+        finish(TEAMS - 1, margin_of[TEAMS - 1])

@@ -14,8 +14,10 @@ P = 128
 C, S, K, Q, L, N = 1024, 256, 6, 16, 8, 128
 KQ = K * Q
 BLOCKS = C // P
-TEAM = 4
-TEAMS = BLOCKS // TEAM
+BANK_BLOCKS = 4
+TEAM_SIZES = (1, 2, 4, 1)
+TEAM_STARTS = (0, 1, 3, 7)
+assert sum(TEAM_SIZES) == BLOCKS and max(TEAM_SIZES) <= BANK_BLOCKS
 FLOPS = 2 * C * K * N
 
 
@@ -26,30 +28,25 @@ def tile_regimerulesnet_kernel(tc, x, th, ineq, esign, mask, tau, offs, out):
     with (
         tc.tile_pool(name="held", bufs=1) as held,
         tc.tile_pool(name="d_pool", bufs=BLOCKS) as d_pool,
-        tc.tile_pool(name="rule_pool", bufs=3) as rule_pool,
+        tc.tile_pool(name="rule_pool", bufs=2 * K) as rule_pool,
         tc.tile_pool(name="out_pool", bufs=2) as out_pool,
-        tc.psum_pool(name="psum_once", bufs=1) as psum_once,
         tc.psum_pool(name="psum_flip", bufs=2) as psum_flip,
         tc.psum_pool(name="psum_margin", bufs=2) as psum_margin,
     ):
         offsets = held.tile([P, N // 16], U16, name="offsets")
         nc.sync.dma_start(offsets[:], offs)
-        x_blocks = []
-        for b in range(BLOCKS):
-            x_block = held.tile([P, S], F32, name=f"x_block{b}")
-            nc.sync.dma_start(x_block[:], x_view[:, b, :])
-            x_blocks.append(x_block)
-
         th0_all = held.tile([P, N], F32, name="th0_all")
-        nc.scalar.dma_start(th0_all[:], th.rearrange("k n -> (k n)")[0:N].partition_broadcast(P))
-        rows = held.tile([P, P], F32, name="rows")
-        nc.vector.memset(rows[:], 0.0)
-        nc.scalar.dma_start(rows[0:K, :], ineq)
-        nc.scalar.dma_start(rows[K : 2 * K, :], esign)
-        nc.scalar.dma_start(rows[2 * K : 3 * K, :], mask)
-        nc.scalar.dma_start(rows[3 * K : 4 * K, :], th)
+        nc.sync.dma_start(th0_all[:], th.rearrange("k n -> (k n)")[0:N].partition_broadcast(P))
+        x_blocks = [held.tile([P, S], F32, name=f"x_block{b}") for b in range(BLOCKS)]
+        nc.sync.dma_start(x_blocks[0][:], x_view[:, 0, :])
+        columns = {}
+        for name, parameter in (("ineq", ineq), ("th", th), ("esign", esign), ("mask", mask)):
+            columns[name] = held.tile([P, K], F32, name=f"{name}_columns")
+            nc.sync.dma_start(columns[name][:], parameter.rearrange("k n -> n k"))
         tau_all = held.tile([P, KQ], F32, name="tau_all")
-        nc.scalar.dma_start(tau_all[:], tau.rearrange("k q -> (k q)").partition_broadcast(P))
+        nc.sync.dma_start(tau_all[:], tau.rearrange("k q -> (k q)").partition_broadcast(P))
+        for b in range(1, BLOCKS):
+            nc.sync.dma_start(x_blocks[b][:], x_view[:, b, :])
 
         identity = held.tile([P, P], F32, name="identity")
         make_identity(nc, identity[:])
@@ -68,30 +65,31 @@ def tile_regimerulesnet_kernel(tc, x, th, ineq, esign, mask, tau, offs, out):
         nc.vector.tensor_scalar_mul(nth0[:], th0_all[:], -1.0)
 
         def look_up(team):
-            flipped = psum_flip.tile([P, TEAM * P], F32, name="flipped")
-            for i in range(TEAM):
+            flipped = psum_flip.tile([P, BANK_BLOCKS * P], F32, name="flipped")
+            for i in range(TEAM_SIZES[team]):
                 d0 = d_pool.tile([P, N], F32, name="d0")
-                nc.vector.tensor_tensor(d0[:], x_blocks[team * TEAM + i][:].indirect(offsets[:]), nth0[:], ADD)
+                nc.vector.tensor_tensor(d0[:], x_blocks[TEAM_STARTS[team] + i][:].indirect(offsets[:]), nth0[:], ADD)
                 nc.tensor.transpose(flipped[:, i * P : (i + 1) * P], d0[:], identity[:])
             return flipped
 
-        def flip_parameters():
-            columns = psum_once.tile([P, P], F32, name="columns")
-            nc.tensor.transpose(columns[:], rows[:], identity[:])
-            gate = held.tile([P, K], F32, name="gate")
-            nc.scalar.activation(gate[:], columns[:, 2 * K : 3 * K], FUNC.Sigmoid)
-            tanhs = held.tile([P, 2 * K], F32, name="tanhs")
-            nc.scalar.activation(tanhs[:], columns[:, 0 : 2 * K], FUNC.Tanh)
-            th_columns = held.tile([P, K], F32, name="th_columns")
-            nc.vector.tensor_copy(th_columns[:], columns[:, 3 * K : 4 * K])
+        def prepare_comparison():
+            slope = held.tile([P, K], F32, name="slope")
+            nc.scalar.activation(slope[:], columns["ineq"][:], FUNC.Tanh)
             above = held.tile([P, K], F32, name="above")
-            nc.vector.tensor_scalar_sub(above[:], th_columns[:], th_columns[:, 0:1])
+            nc.vector.tensor_scalar_sub(above[:], columns["th"][:], columns["th"][:, 0:1])
             steep = held.tile([P, K], F32, name="steep")
-            nc.vector.tensor_scalar_mul(steep[:], tanhs[:, 0:K], 3.0)
+            nc.vector.tensor_scalar_mul(steep[:], slope[:], 3.0)
             shift = held.tile([P, K], F32, name="shift")
-            nc.vector.scalar_tensor_tensor(shift[:], above[:], -3.0, tanhs[:, 0:K], MULT, MULT)
+            nc.vector.scalar_tensor_tensor(shift[:], above[:], -3.0, slope[:], MULT, MULT)
+            return steep, shift
+
+        def prepare_weights():
+            sign = held.tile([P, K], F32, name="sign")
+            nc.scalar.activation(sign[:], columns["esign"][:], FUNC.Tanh)
+            gate = held.tile([P, K], F32, name="gate")
+            nc.scalar.activation(gate[:], columns["mask"][:], FUNC.Sigmoid)
             a = held.tile([P, K], F32, name="a")
-            nc.vector.tensor_tensor(a[:], gate[:], tanhs[:, K : 2 * K], MULT)
+            nc.vector.tensor_tensor(a[:], gate[:], sign[:], MULT)
             weights = held.tile([P, KQ], BF16, name="weights")
             nc.vector.tensor_tensor(
                 weights[:].rearrange("p (k q) -> p k q", q=Q),
@@ -99,7 +97,7 @@ def tile_regimerulesnet_kernel(tc, x, th, ineq, esign, mask, tau, offs, out):
                 a[:].unsqueeze(2).to_broadcast([P, K, Q]),
                 MULT,
             )
-            return steep, shift, weights
+            return weights
 
         def split_tau():
             tau_high = held.tile([P, KQ], BF16, name="tau_high")
@@ -108,47 +106,62 @@ def tile_regimerulesnet_kernel(tc, x, th, ineq, esign, mask, tau, offs, out):
             nc.vector.tensor_tensor(tau_low[:], tau_all[:], tau_high[:], SUBTRACT)
             return tau_high, tau_low
 
-        def open_margin():
-            margin = psum_margin.tile([P, TEAM * KQ], F32, name="margin")
+        def open_margin(team):
+            size = TEAM_SIZES[team]
+            margin = psum_margin.tile([P, BANK_BLOCKS * KQ], F32, name="margin")
             for t, term in enumerate(tau_terms):
                 nc.tensor.matmul(
-                    margin[:].rearrange("p (i f) -> p i f", f=KQ),
+                    margin[:, 0 : size * KQ].rearrange("p (i f) -> p i f", f=KQ),
                     lhsT=minus_share[:],
-                    rhs=term[:].unsqueeze(1).to_broadcast([P, TEAM, KQ]),
+                    rhs=term[:].unsqueeze(1).to_broadcast([P, size, KQ]),
                     start=(t == 0),
                     stop=False,
                 )
             return margin
 
-        def compare_and_weigh(k, flipped, margin):
-            rule = rule_pool.tile([P, TEAM * P], BF16, name="rule")
-            nc.scalar.activation(rule[:], flipped[:], FUNC.Tanh, scale=steep[:, k : k + 1], bias=shift[:, k : k + 1])
-            for i in range(TEAM):
+        def compare(team, k, flipped):
+            width = TEAM_SIZES[team] * P
+            rule = rule_pool.tile([P, BANK_BLOCKS * P], BF16, name="rule")
+            nc.scalar.activation(
+                rule[:, 0:width], flipped[:, 0:width], FUNC.Tanh, scale=steep[:, k : k + 1], bias=shift[:, k : k + 1]
+            )
+            return rule
+
+        def weigh(team, k, rule, margin):
+            size = TEAM_SIZES[team]
+            for i in range(size):
                 nc.tensor.matmul(
                     margin[:, i * KQ + k * Q : i * KQ + (k + 1) * Q],
                     lhsT=rule[:, i * P : (i + 1) * P],
                     rhs=weights[:, k * Q : (k + 1) * Q],
                     start=False,
-                    stop=(k == K - 1 and i == TEAM - 1),
+                    stop=(k == K - 1 and i == size - 1),
                 )
 
         def finish(team, margin):
-            active = out_pool.tile([P, TEAM * KQ], F32, name="active")
-            nc.scalar.activation(active[:], margin[:], FUNC.Sigmoid, scale=6.0)
+            size = TEAM_SIZES[team]
+            active = out_pool.tile([P, BANK_BLOCKS * KQ], F32, name="active")
+            nc.scalar.activation(active[:, 0 : size * KQ], margin[:, 0 : size * KQ], FUNC.Sigmoid, scale=6.0)
             nc.sync.dma_start(
-                out_view[:, team * TEAM : (team + 1) * TEAM, :], active[:].rearrange("p (i f) -> p i f", f=KQ)
+                out_view[:, TEAM_STARTS[team] : TEAM_STARTS[team] + size, :],
+                active[:, 0 : size * KQ].rearrange("p (i f) -> p i f", f=KQ),
             )
 
+        teams = len(TEAM_SIZES)
         flipped_of = {0: look_up(0)}
-        steep, shift, weights = flip_parameters()
-        tau_terms = split_tau()
+        steep, shift = prepare_comparison()
         margin_of = {}
-        for team in range(TEAMS):
-            if team + 1 < TEAMS:
-                flipped_of[team + 1] = look_up(team + 1)
-            margin_of[team] = open_margin()
+        for team in range(teams):
             for k in range(K):
-                compare_and_weigh(k, flipped_of[team], margin_of[team])
-                if k == 0 and team > 0:
-                    finish(team - 1, margin_of[team - 1])
-        finish(TEAMS - 1, margin_of[TEAMS - 1])
+                rule = compare(team, k, flipped_of[team])
+                if k == 0:
+                    if team == 0:
+                        weights = prepare_weights()
+                        tau_terms = split_tau()
+                    else:
+                        finish(team - 1, margin_of[team - 1])
+                    if team + 1 < teams:
+                        flipped_of[team + 1] = look_up(team + 1)
+                    margin_of[team] = open_margin(team)
+                weigh(team, k, rule, margin_of[team])
+        finish(teams - 1, margin_of[teams - 1])

@@ -61,6 +61,11 @@ def tile_regimerulesnet_kernel(tc, x, th, ineq, esign, mask, tau, offs, out):
         minus_share = held.tile([P, P], BF16, name="minus_share")
         nc.gpsimd.memset(minus_share[:], -1.0 / P)
 
+        warm_in = held.tile([P, 1], F32, name="warm_in")
+        nc.vector.memset(warm_in[:], 0.0)
+        warm_out = held.tile([P, 1], F32, name="warm_out")
+        nc.scalar.activation(warm_out[:], warm_in[:], FUNC.Sigmoid)
+
         nth0 = held.tile([P, N], F32, name="nth0")
         nc.vector.tensor_scalar_mul(nth0[:], th0_all[:], -1.0)
 

@@ -33,20 +33,30 @@ def tile_regimerulesnet_kernel(tc, x, th, ineq, esign, mask, tau, offs, out):
         tc.psum_pool(name="psum_flip", bufs=2) as psum_flip,
         tc.psum_pool(name="psum_margin", bufs=2) as psum_margin,
     ):
+        x_blocks = [held.tile([P, S], F32, name=f"x_block{b}") for b in range(BLOCKS)]
+        columns = {}
+
+        def load_blocks(first, end):
+            for b in range(first, end):
+                nc.sync.dma_start(x_blocks[b][:], x_view[:, b, :])
+
+        def load_columns(name, parameter):
+            columns[name] = held.tile([P, K], F32, name=f"{name}_columns")
+            nc.sync.dma_start(columns[name][:], parameter.rearrange("k n -> n k"))
+
+        tau_all = held.tile([P, KQ], F32, name="tau_all")
+        nc.sync.dma_start(tau_all[:], tau.rearrange("k q -> (k q)").partition_broadcast(P))
         offsets = held.tile([P, N // 16], U16, name="offsets")
         nc.sync.dma_start(offsets[:], offs)
         th0_all = held.tile([P, N], F32, name="th0_all")
         nc.sync.dma_start(th0_all[:], th.rearrange("k n -> (k n)")[0:N].partition_broadcast(P))
-        x_blocks = [held.tile([P, S], F32, name=f"x_block{b}") for b in range(BLOCKS)]
-        nc.sync.dma_start(x_blocks[0][:], x_view[:, 0, :])
-        columns = {}
-        for name, parameter in (("ineq", ineq), ("th", th), ("esign", esign), ("mask", mask)):
-            columns[name] = held.tile([P, K], F32, name=f"{name}_columns")
-            nc.sync.dma_start(columns[name][:], parameter.rearrange("k n -> n k"))
-        tau_all = held.tile([P, KQ], F32, name="tau_all")
-        nc.sync.dma_start(tau_all[:], tau.rearrange("k q -> (k q)").partition_broadcast(P))
-        for b in range(1, BLOCKS):
-            nc.sync.dma_start(x_blocks[b][:], x_view[:, b, :])
+        load_blocks(0, TEAM_STARTS[1])
+        load_columns("ineq", ineq)
+        load_columns("th", th)
+        load_blocks(TEAM_STARTS[1], TEAM_STARTS[2])
+        load_columns("esign", esign)
+        load_columns("mask", mask)
+        load_blocks(TEAM_STARTS[2], BLOCKS)
 
         identity = held.tile([P, P], F32, name="identity")
         make_identity(nc, identity[:])
@@ -80,12 +90,14 @@ def tile_regimerulesnet_kernel(tc, x, th, ineq, esign, mask, tau, offs, out):
         def prepare_comparison():
             slope = held.tile([P, K], F32, name="slope")
             nc.scalar.activation(slope[:], columns["ineq"][:], FUNC.Tanh)
-            above = held.tile([P, K], F32, name="above")
-            nc.vector.tensor_scalar_sub(above[:], columns["th"][:], columns["th"][:, 0:1])
             steep = held.tile([P, K], F32, name="steep")
             nc.vector.tensor_scalar_mul(steep[:], slope[:], 3.0)
+            minus_steep = held.tile([P, K], F32, name="minus_steep")
+            nc.vector.tensor_scalar_mul(minus_steep[:], slope[:], -3.0)
             shift = held.tile([P, K], F32, name="shift")
-            nc.vector.scalar_tensor_tensor(shift[:], above[:], -3.0, slope[:], MULT, MULT)
+            nc.vector.scalar_tensor_tensor(
+                shift[:], columns["th"][:], columns["th"][:, 0:1], minus_steep[:], SUBTRACT, MULT
+            )
             return steep, shift
 
         def prepare_weights():
@@ -153,20 +165,22 @@ def tile_regimerulesnet_kernel(tc, x, th, ineq, esign, mask, tau, offs, out):
             )
 
         teams = len(TEAM_SIZES)
+        tau_terms = split_tau()
         flipped_of = {0: look_up(0)}
         steep, shift = prepare_comparison()
+        flipped_of[1] = look_up(1)
         margin_of = {}
         for team in range(teams):
+            rules = []
             for k in range(K):
-                rule = compare(team, k, flipped_of[team])
-                if k == 0:
-                    if team == 0:
-                        weights = prepare_weights()
-                        tau_terms = split_tau()
-                    else:
-                        finish(team - 1, margin_of[team - 1])
-                    if team + 1 < teams:
-                        flipped_of[team + 1] = look_up(team + 1)
-                    margin_of[team] = open_margin(team)
-                weigh(team, k, rule, margin_of[team])
+                rules.append(compare(team, k, flipped_of[team]))
+                if k == 2 and team > 0:
+                    finish(team - 1, margin_of[team - 1])
+            if team == 0:
+                weights = prepare_weights()
+            margin_of[team] = open_margin(team)
+            for k in range(K):
+                weigh(team, k, rules[k], margin_of[team])
+            if team + 2 < teams:
+                flipped_of[team + 2] = look_up(team + 2)
         finish(teams - 1, margin_of[teams - 1])

@@ -11,6 +11,7 @@ IS_GE = mybir.AluOpType.is_ge
 FUNC = mybir.ActivationFunctionType
 
 P = 128
+HALF = P // 2
 C, S, K, Q, L, N = 1024, 256, 6, 16, 8, 128
 KQ = K * Q
 BLOCKS = C // P
@@ -69,7 +70,7 @@ def tile_regimerulesnet_kernel(tc, x, th, ineq, esign, mask, tau, offs, out):
             out=in_group[:], in_=in_group[:], pattern=[[L, Q]], compare_op=IS_GE, fill=0.0, base=L - 1, channel_multiplier=-1
         )
         minus_share = held.tile([P, P], BF16, name="minus_share")
-        nc.gpsimd.memset(minus_share[:], -1.0 / P)
+        nc.gpsimd.memset(minus_share[:], -1.0 / HALF)
 
         warm_in = held.tile([P, 1], F32, name="warm_in")
         nc.vector.memset(warm_in[:], 0.0)
@@ -119,21 +120,21 @@ def tile_regimerulesnet_kernel(tc, x, th, ineq, esign, mask, tau, offs, out):
         def split_tau():
             tau_high = held.tile([P, KQ], BF16, name="tau_high")
             nc.vector.tensor_copy(tau_high[:], tau_all[:])
-            tau_low = held.tile([P, KQ], BF16, name="tau_low")
-            nc.vector.tensor_tensor(tau_low[:], tau_all[:], tau_high[:], SUBTRACT)
-            return tau_high, tau_low
+            tau_terms = held.tile([P, KQ], BF16, name="tau_terms")
+            nc.vector.tensor_copy(tau_terms[0:HALF, :], tau_all[0:HALF, :])
+            nc.vector.tensor_tensor(tau_terms[HALF:P, :], tau_all[HALF:P, :], tau_high[HALF:P, :], SUBTRACT)
+            return tau_terms
 
         def open_margin(team):
             size = TEAM_SIZES[team]
             margin = psum_margin.tile([P, BANK_BLOCKS * KQ], F32, name="margin")
-            for t, term in enumerate(tau_terms):
-                nc.tensor.matmul(
-                    margin[:, 0 : size * KQ].rearrange("p (i f) -> p i f", f=KQ),
-                    lhsT=minus_share[:],
-                    rhs=term[:].unsqueeze(1).to_broadcast([P, size, KQ]),
-                    start=(t == 0),
-                    stop=False,
-                )
+            nc.tensor.matmul(
+                margin[:, 0 : size * KQ].rearrange("p (i f) -> p i f", f=KQ),
+                lhsT=minus_share[:],
+                rhs=tau_terms[:].unsqueeze(1).to_broadcast([P, size, KQ]),
+                start=True,
+                stop=False,
+            )
             return margin
 
         def compare(team, k, flipped):

@@ -29,7 +29,7 @@ def tile_regimerulesnet_kernel(tc, x, th, ineq, esign, mask, tau, offs, out):
     with (
         tc.tile_pool(name="held", bufs=1) as held,
         tc.tile_pool(name="d_pool", bufs=BLOCKS) as d_pool,
-        tc.tile_pool(name="rule_pool", bufs=2 * K) as rule_pool,
+        tc.tile_pool(name="rule_pool", bufs=len(TEAM_SIZES) * K) as rule_pool,
         tc.tile_pool(name="out_pool", bufs=2) as out_pool,
         tc.psum_pool(name="psum_flip", bufs=2) as psum_flip,
         tc.psum_pool(name="psum_margin", bufs=2) as psum_margin,

@@ -16,9 +16,13 @@ C, S, K, Q, L, N = 1024, 256, 6, 16, 8, 128
 KQ = K * Q
 BLOCKS = C // P
 BANK_BLOCKS = 4
-TEAM_SIZES = (1, 2, 4, 1)
-TEAM_STARTS = (0, 1, 3, 7)
+TEAM_SIZES = (1, 2, 3, 2)
+TEAM_STARTS = (0, 1, 3, 6)
 assert sum(TEAM_SIZES) == BLOCKS and max(TEAM_SIZES) <= BANK_BLOCKS
+BATCHES = ((0, 1), (2,), (3,))
+BATCH_STARTS = tuple(TEAM_STARTS[teams[0]] for teams in BATCHES)
+BATCH_SIZES = tuple(sum(TEAM_SIZES[team] for team in teams) for teams in BATCHES)
+assert max(BATCH_SIZES) <= BANK_BLOCKS
 FLOPS = 2 * C * K * N
 
 
@@ -28,10 +32,11 @@ def tile_regimerulesnet_kernel(tc, x, th, ineq, esign, mask, tau, offs, out):
     out_view = out.rearrange("(p b) f -> p b f", b=BLOCKS)
     with (
         tc.tile_pool(name="held", bufs=1) as held,
+        tc.tile_pool(name="turn_pool", bufs=1) as turn_pool,
         tc.tile_pool(name="d_pool", bufs=BLOCKS) as d_pool,
         tc.tile_pool(name="rule_pool", bufs=len(TEAM_SIZES) * K) as rule_pool,
-        tc.tile_pool(name="out_pool", bufs=2) as out_pool,
-        tc.psum_pool(name="psum_flip", bufs=2) as psum_flip,
+        tc.tile_pool(name="out_pool", bufs=len(BATCHES)) as out_pool,
+        tc.psum_pool(name="psum_flip", bufs=3) as psum_flip,
         tc.psum_pool(name="psum_margin", bufs=2) as psum_margin,
     ):
         x_blocks = [held.tile([P, S], F32, name=f"x_block{b}") for b in range(BLOCKS)]
@@ -45,8 +50,6 @@ def tile_regimerulesnet_kernel(tc, x, th, ineq, esign, mask, tau, offs, out):
             columns[name] = held.tile([P, K], F32, name=f"{name}_columns")
             nc.sync.dma_start(columns[name][:], parameter.rearrange("k n -> n k"))
 
-        tau_all = held.tile([P, KQ], F32, name="tau_all")
-        nc.sync.dma_start(tau_all[:], tau.rearrange("k q -> (k q)").partition_broadcast(P))
         offsets = held.tile([P, N // 16], U16, name="offsets")
         nc.sync.dma_start(offsets[:], offs)
         th0_all = held.tile([P, N], F32, name="th0_all")
@@ -57,7 +60,10 @@ def tile_regimerulesnet_kernel(tc, x, th, ineq, esign, mask, tau, offs, out):
         load_blocks(TEAM_STARTS[1], TEAM_STARTS[2])
         load_columns("esign", esign)
         load_columns("mask", mask)
-        load_blocks(TEAM_STARTS[2], BLOCKS)
+        load_blocks(TEAM_STARTS[2], TEAM_STARTS[3])
+        tau_all = held.tile([P, KQ], F32, name="tau_all")
+        nc.sync.dma_start(tau_all[:], tau.rearrange("k q -> (k q)").partition_broadcast(P))
+        load_blocks(TEAM_STARTS[3], BLOCKS)
 
         identity = held.tile([P, P], F32, name="identity")
         make_identity(nc, identity[:])
@@ -83,7 +89,7 @@ def tile_regimerulesnet_kernel(tc, x, th, ineq, esign, mask, tau, offs, out):
         def look_up(team):
             flipped = psum_flip.tile([P, BANK_BLOCKS * P], F32, name="flipped")
             for i in range(TEAM_SIZES[team]):
-                d0 = d_pool.tile([P, N], F32, name="d0")
+                d0 = (turn_pool if team == 0 else d_pool).tile([P, N], F32, name="d0", tag="turn")
                 nc.vector.tensor_tensor(d0[:], x_blocks[TEAM_STARTS[team] + i][:].indirect(offsets[:]), nth0[:], ADD)
                 nc.tensor.transpose(flipped[:, i * P : (i + 1) * P], d0[:], identity[:])
             return flipped
@@ -102,12 +108,12 @@ def tile_regimerulesnet_kernel(tc, x, th, ineq, esign, mask, tau, offs, out):
             return steep, shift
 
         def prepare_weights():
-            sign = held.tile([P, K], F32, name="sign")
-            nc.scalar.activation(sign[:], columns["esign"][:], FUNC.Tanh)
-            gate = held.tile([P, K], F32, name="gate")
-            nc.scalar.activation(gate[:], columns["mask"][:], FUNC.Sigmoid)
+            factors = turn_pool.tile([P, N], F32, name="factors", tag="turn")
+            sign, gate = factors[:, 0:K], factors[:, K : 2 * K]
+            nc.scalar.activation(sign, columns["esign"][:], FUNC.Tanh)
+            nc.scalar.activation(gate, columns["mask"][:], FUNC.Sigmoid)
             a = held.tile([P, K], F32, name="a")
-            nc.vector.tensor_tensor(a[:], gate[:], sign[:], MULT)
+            nc.vector.tensor_tensor(a[:], gate, sign, MULT)
             weights = held.tile([P, KQ], BF16, name="weights")
             nc.vector.tensor_tensor(
                 weights[:].rearrange("p (k q) -> p k q", q=Q),
@@ -118,15 +124,13 @@ def tile_regimerulesnet_kernel(tc, x, th, ineq, esign, mask, tau, offs, out):
             return weights
 
         def split_tau():
-            tau_high = held.tile([P, KQ], BF16, name="tau_high")
-            nc.vector.tensor_copy(tau_high[:], tau_all[:])
             tau_terms = held.tile([P, KQ], BF16, name="tau_terms")
-            nc.vector.tensor_copy(tau_terms[0:HALF, :], tau_all[0:HALF, :])
-            nc.vector.tensor_tensor(tau_terms[HALF:P, :], tau_all[HALF:P, :], tau_high[HALF:P, :], SUBTRACT)
+            nc.vector.tensor_copy(tau_terms[:], tau_all[:])
+            nc.vector.tensor_tensor(tau_terms[HALF:P, :], tau_all[HALF:P, :], tau_terms[HALF:P, :], SUBTRACT)
             return tau_terms
 
-        def open_margin(team):
-            size = TEAM_SIZES[team]
+        def open_margin(batch):
+            size = BATCH_SIZES[batch]
             margin = psum_margin.tile([P, BANK_BLOCKS * KQ], F32, name="margin")
             nc.tensor.matmul(
                 margin[:, 0 : size * KQ].rearrange("p (i f) -> p i f", f=KQ),
@@ -145,43 +149,46 @@ def tile_regimerulesnet_kernel(tc, x, th, ineq, esign, mask, tau, offs, out):
             )
             return rule
 
-        def weigh(team, k, rule, margin):
-            size = TEAM_SIZES[team]
-            for i in range(size):
+        def weigh(batch, team, k, rule, margin):
+            for i in range(TEAM_SIZES[team]):
+                i_batch = TEAM_STARTS[team] + i - BATCH_STARTS[batch]
                 nc.tensor.matmul(
-                    margin[:, i * KQ + k * Q : i * KQ + (k + 1) * Q],
+                    margin[:, i_batch * KQ + k * Q : i_batch * KQ + (k + 1) * Q],
                     lhsT=rule[:, i * P : (i + 1) * P],
                     rhs=weights[:, k * Q : (k + 1) * Q],
                     start=False,
-                    stop=(k == K - 1 and i == size - 1),
+                    stop=(k == K - 1 and i_batch == BATCH_SIZES[batch] - 1),
                 )
 
-        def finish(team, margin):
-            size = TEAM_SIZES[team]
+        def finish(batch, margin):
+            size = BATCH_SIZES[batch]
             active = out_pool.tile([P, BANK_BLOCKS * KQ], F32, name="active")
             nc.scalar.activation(active[:, 0 : size * KQ], margin[:, 0 : size * KQ], FUNC.Sigmoid, scale=6.0)
             nc.sync.dma_start(
-                out_view[:, TEAM_STARTS[team] : TEAM_STARTS[team] + size, :],
+                out_view[:, BATCH_STARTS[batch] : BATCH_STARTS[batch] + size, :],
                 active[:, 0 : size * KQ].rearrange("p (i f) -> p i f", f=KQ),
             )
 
         teams = len(TEAM_SIZES)
-        tau_terms = split_tau()
         flipped_of = {0: look_up(0)}
         steep, shift = prepare_comparison()
         flipped_of[1] = look_up(1)
         margin_of = {}
-        for team in range(teams):
-            rules = []
-            for k in range(K):
-                rules.append(compare(team, k, flipped_of[team]))
-                if k == 2 and team > 0:
-                    finish(team - 1, margin_of[team - 1])
-            if team == 0:
-                weights = prepare_weights()
-            margin_of[team] = open_margin(team)
-            for k in range(K):
-                weigh(team, k, rules[k], margin_of[team])
-            if team + 2 < teams:
-                flipped_of[team + 2] = look_up(team + 2)
-        finish(teams - 1, margin_of[teams - 1])
+        for batch in range(len(BATCHES)):
+            for team in BATCHES[batch]:
+                rules = []
+                for k in range(K):
+                    rules.append(compare(team, k, flipped_of[team]))
+                if team == BATCHES[batch][0] and batch > 0:
+                    finish(batch - 1, margin_of[batch - 1])
+                if team == 0:
+                    weights = prepare_weights()
+                    flipped_of[2] = look_up(2)
+                    tau_terms = split_tau()
+                if team == BATCHES[batch][0]:
+                    margin_of[batch] = open_margin(batch)
+                for k in range(K):
+                    weigh(batch, team, k, rules[k], margin_of[batch])
+                if team + 3 < teams:
+                    flipped_of[team + 3] = look_up(team + 3)
+        finish(len(BATCHES) - 1, margin_of[len(BATCHES) - 1])

@@ -56,8 +56,9 @@ def tile_regimerulesnet_kernel(tc, x, th, ineq, esign, mask, tau, offs, out):
         nc.sync.dma_start(th0_all[:], th.rearrange("k n -> (k n)")[0:N].partition_broadcast(P))
         load_blocks(0, TEAM_STARTS[1])
         load_columns("ineq", ineq)
+        load_blocks(TEAM_STARTS[1], TEAM_STARTS[1] + 1)
         load_columns("th", th)
-        load_blocks(TEAM_STARTS[1], TEAM_STARTS[2])
+        load_blocks(TEAM_STARTS[1] + 1, TEAM_STARTS[2])
         load_columns("esign", esign)
         load_columns("mask", mask)
         load_blocks(TEAM_STARTS[2], TEAM_STARTS[3])
@@ -144,8 +145,9 @@ def tile_regimerulesnet_kernel(tc, x, th, ineq, esign, mask, tau, offs, out):
         def compare(team, k, flipped):
             width = TEAM_SIZES[team] * P
             rule = rule_pool.tile([P, BANK_BLOCKS * P], BF16, name="rule")
+            bias = 0.0 if k == 0 else shift[:, k : k + 1]
             nc.scalar.activation(
-                rule[:, 0:width], flipped[:, 0:width], FUNC.Tanh, scale=steep[:, k : k + 1], bias=shift[:, k : k + 1]
+                rule[:, 0:width], flipped[:, 0:width], FUNC.Tanh, scale=steep[:, k : k + 1], bias=bias
             )
             return rule
 

@@ -58,10 +58,9 @@ def tile_regimerulesnet_kernel(tc, x, th, ineq, esign, mask, tau, offs, out):
         load_columns("ineq", ineq)
         load_blocks(TEAM_STARTS[1], TEAM_STARTS[1] + 1)
         load_columns("th", th)
-        load_blocks(TEAM_STARTS[1] + 1, TEAM_STARTS[2])
+        load_blocks(TEAM_STARTS[1] + 1, TEAM_STARTS[3])
         load_columns("esign", esign)
         load_columns("mask", mask)
-        load_blocks(TEAM_STARTS[2], TEAM_STARTS[3])
         tau_all = held.tile([P, KQ], F32, name="tau_all")
         nc.sync.dma_start(tau_all[:], tau.rearrange("k q -> (k q)").partition_broadcast(P))
         load_blocks(TEAM_STARTS[3], BLOCKS)

@@ -58,9 +58,10 @@ def tile_regimerulesnet_kernel(tc, x, th, ineq, esign, mask, tau, offs, out):
         load_columns("ineq", ineq)
         load_blocks(TEAM_STARTS[1], TEAM_STARTS[1] + 1)
         load_columns("th", th)
-        load_blocks(TEAM_STARTS[1] + 1, TEAM_STARTS[3])
+        load_blocks(TEAM_STARTS[1] + 1, TEAM_STARTS[3] - 1)
         load_columns("esign", esign)
         load_columns("mask", mask)
+        load_blocks(TEAM_STARTS[3] - 1, TEAM_STARTS[3])
         tau_all = held.tile([P, KQ], F32, name="tau_all")
         nc.sync.dma_start(tau_all[:], tau.rearrange("k q -> (k q)").partition_broadcast(P))
         load_blocks(TEAM_STARTS[3], BLOCKS)
@@ -170,26 +171,27 @@ def tile_regimerulesnet_kernel(tc, x, th, ineq, esign, mask, tau, offs, out):
                 active[:, 0 : size * KQ].rearrange("p (i f) -> p i f", f=KQ),
             )
 
-        teams = len(TEAM_SIZES)
         flipped_of = {0: look_up(0)}
         steep, shift = prepare_comparison()
         flipped_of[1] = look_up(1)
         margin_of = {}
         for batch in range(len(BATCHES)):
+            rules = {}
             for team in BATCHES[batch]:
-                rules = []
                 for k in range(K):
-                    rules.append(compare(team, k, flipped_of[team]))
-                if team == BATCHES[batch][0] and batch > 0:
-                    finish(batch - 1, margin_of[batch - 1])
+                    rules[team, k] = compare(team, k, flipped_of[team])
+                    if team == 1 and k == K // 2 - 1:
+                        weights = prepare_weights()
                 if team == 0:
-                    weights = prepare_weights()
                     flipped_of[2] = look_up(2)
+                if team == 1:
                     tau_terms = split_tau()
-                if team == BATCHES[batch][0]:
-                    margin_of[batch] = open_margin(batch)
+                if batch > 0:
+                    finish(batch - 1, margin_of[batch - 1])
+            margin_of[batch] = open_margin(batch)
+            for team in BATCHES[batch]:
                 for k in range(K):
-                    weigh(batch, team, k, rules[k], margin_of[batch])
-                if team + 3 < teams:
-                    flipped_of[team + 3] = look_up(team + 3)
+                    weigh(batch, team, k, rules[team, k], margin_of[batch])
+            if batch == 0:
+                flipped_of[3] = look_up(3)
         finish(len(BATCHES) - 1, margin_of[len(BATCHES) - 1])

@@ -37,7 +37,7 @@ def tile_regimerulesnet_kernel(tc, x, th, ineq, esign, mask, tau, offs, out):
         tc.tile_pool(name="rule_pool", bufs=len(TEAM_SIZES) * K) as rule_pool,
         tc.tile_pool(name="out_pool", bufs=len(BATCHES)) as out_pool,
         tc.psum_pool(name="psum_flip", bufs=3) as psum_flip,
-        tc.psum_pool(name="psum_margin", bufs=2) as psum_margin,
+        tc.psum_pool(name="psum_margin", bufs=len(BATCHES)) as psum_margin,
     ):
         x_blocks = [held.tile([P, S], F32, name=f"x_block{b}") for b in range(BLOCKS)]
         columns = {}
@@ -182,11 +182,13 @@ def tile_regimerulesnet_kernel(tc, x, th, ineq, esign, mask, tau, offs, out):
                     rules[team, k] = compare(team, k, flipped_of[team])
                     if team == 1 and k == K // 2 - 1:
                         weights = prepare_weights()
+                    if batch == len(BATCHES) - 1 and k == K // 2 - 1:
+                        finish(0, margin_of[0])
                 if team == 0:
                     flipped_of[2] = look_up(2)
                 if team == 1:
                     tau_terms = split_tau()
-                if batch > 0:
+                if batch == len(BATCHES) - 1:
                     finish(batch - 1, margin_of[batch - 1])
             margin_of[batch] = open_margin(batch)
             for team in BATCHES[batch]:

import concourse.mybir as mybir
from concourse.masks import make_identity

F32 = mybir.dt.float32
BF16 = mybir.dt.bfloat16
U16 = mybir.dt.uint16
ADD = mybir.AluOpType.add
SUBTRACT = mybir.AluOpType.subtract
MULT = mybir.AluOpType.mult
IS_GE = mybir.AluOpType.is_ge
FUNC = mybir.ActivationFunctionType

P = 128
HALF = P // 2
C, S, K, Q, L, N = 1024, 256, 6, 16, 8, 128
KQ = K * Q
BLOCKS = C // P
BANK_BLOCKS = 4
TEAM_SIZES = (1, 2, 3, 2)
TEAM_STARTS = (0, 1, 3, 6)
assert sum(TEAM_SIZES) == BLOCKS and max(TEAM_SIZES) <= BANK_BLOCKS
BATCHES = ((0, 1), (2,), (3,))
BATCH_STARTS = tuple(TEAM_STARTS[teams[0]] for teams in BATCHES)
BATCH_SIZES = tuple(sum(TEAM_SIZES[team] for team in teams) for teams in BATCHES)
assert max(BATCH_SIZES) <= BANK_BLOCKS
FLOPS = 2 * C * K * N


def tile_regimerulesnet_kernel(tc, x, th, ineq, esign, mask, tau, offs, out):
    nc = tc.nc
    x_view = x.rearrange("(p b) s -> p b s", b=BLOCKS)
    out_view = out.rearrange("(p b) f -> p b f", b=BLOCKS)
    with (
        tc.tile_pool(name="held", bufs=1) as held,
        tc.tile_pool(name="turn_pool", bufs=1) as turn_pool,
        tc.tile_pool(name="d_pool", bufs=BLOCKS) as d_pool,
        tc.tile_pool(name="rule_pool", bufs=len(TEAM_SIZES) * K) as rule_pool,
        tc.tile_pool(name="out_pool", bufs=len(BATCHES)) as out_pool,
        tc.psum_pool(name="psum_flip", bufs=3) as psum_flip,
        tc.psum_pool(name="psum_margin", bufs=len(BATCHES)) as psum_margin,
    ):
        x_blocks = [held.tile([P, S], F32, name=f"x_block{b}") for b in range(BLOCKS)]
        columns = {}

        def load_blocks(first, end):
            for b in range(first, end):
                nc.sync.dma_start(x_blocks[b][:], x_view[:, b, :])

        def load_columns(name, parameter):
            columns[name] = held.tile([P, K], F32, name=f"{name}_columns")
            nc.sync.dma_start(columns[name][:], parameter.rearrange("k n -> n k"))

        offsets = held.tile([P, N // 16], U16, name="offsets")
        nc.sync.dma_start(offsets[:], offs)
        th0_all = held.tile([P, N], F32, name="th0_all")
        nc.sync.dma_start(th0_all[:], th.rearrange("k n -> (k n)")[0:N].partition_broadcast(P))
        load_blocks(0, TEAM_STARTS[1])
        load_columns("ineq", ineq)
        load_blocks(TEAM_STARTS[1], TEAM_STARTS[1] + 1)
        load_columns("th", th)
        load_blocks(TEAM_STARTS[1] + 1, TEAM_STARTS[3] - 1)
        load_columns("esign", esign)
        load_columns("mask", mask)
        load_blocks(TEAM_STARTS[3] - 1, TEAM_STARTS[3])
        tau_all = held.tile([P, KQ], F32, name="tau_all")
        nc.sync.dma_start(tau_all[:], tau.rearrange("k q -> (k q)").partition_broadcast(P))
        load_blocks(TEAM_STARTS[3], BLOCKS)

        identity = held.tile([P, P], F32, name="identity")
        make_identity(nc, identity[:])
        in_group = held.tile([P, Q], F32, name="in_group")
        nc.gpsimd.memset(in_group[:], 1.0)
        nc.gpsimd.affine_select(
            out=in_group[:], in_=in_group[:], pattern=[[-L, Q]], compare_op=IS_GE, fill=0.0, base=0, channel_multiplier=1
        )
        nc.gpsimd.affine_select(
            out=in_group[:], in_=in_group[:], pattern=[[L, Q]], compare_op=IS_GE, fill=0.0, base=L - 1, channel_multiplier=-1
        )
        minus_share = held.tile([P, P], BF16, name="minus_share")
        nc.gpsimd.memset(minus_share[:], -1.0 / HALF)

        warm_in = held.tile([P, 1], F32, name="warm_in")
        nc.vector.memset(warm_in[:], 0.0)
        warm_out = held.tile([P, 1], F32, name="warm_out")
        nc.scalar.activation(warm_out[:], warm_in[:], FUNC.Sigmoid)

        nth0 = held.tile([P, N], F32, name="nth0")
        nc.vector.tensor_scalar_mul(nth0[:], th0_all[:], -1.0)

        def look_up(team):
            flipped = psum_flip.tile([P, BANK_BLOCKS * P], F32, name="flipped")
            for i in range(TEAM_SIZES[team]):
                d0 = (turn_pool if team == 0 else d_pool).tile([P, N], F32, name="d0", tag="turn")
                nc.vector.tensor_tensor(d0[:], x_blocks[TEAM_STARTS[team] + i][:].indirect(offsets[:]), nth0[:], ADD)
                nc.tensor.transpose(flipped[:, i * P : (i + 1) * P], d0[:], identity[:])
            return flipped

        def prepare_comparison():
            slope = held.tile([P, K], F32, name="slope")
            nc.scalar.activation(slope[:], columns["ineq"][:], FUNC.Tanh)
            steep = held.tile([P, K], F32, name="steep")
            nc.vector.tensor_scalar_mul(steep[:], slope[:], 3.0)
            minus_steep = held.tile([P, K], F32, name="minus_steep")
            nc.vector.tensor_scalar_mul(minus_steep[:], slope[:], -3.0)
            shift = held.tile([P, K], F32, name="shift")
            nc.vector.scalar_tensor_tensor(
                shift[:], columns["th"][:], columns["th"][:, 0:1], minus_steep[:], SUBTRACT, MULT
            )
            return steep, shift

        def prepare_weights():
            factors = turn_pool.tile([P, N], F32, name="factors", tag="turn")
            sign, gate = factors[:, 0:K], factors[:, K : 2 * K]
            nc.scalar.activation(sign, columns["esign"][:], FUNC.Tanh)
            nc.scalar.activation(gate, columns["mask"][:], FUNC.Sigmoid)
            a = held.tile([P, K], F32, name="a")
            nc.vector.tensor_tensor(a[:], gate, sign, MULT)
            weights = held.tile([P, KQ], BF16, name="weights")
            nc.vector.tensor_tensor(
                weights[:].rearrange("p (k q) -> p k q", q=Q),
                in_group[:].unsqueeze(1).to_broadcast([P, K, Q]),
                a[:].unsqueeze(2).to_broadcast([P, K, Q]),
                MULT,
            )
            return weights

        def split_tau():
            tau_terms = held.tile([P, KQ], BF16, name="tau_terms")
            nc.vector.tensor_copy(tau_terms[:], tau_all[:])
            nc.vector.tensor_tensor(tau_terms[HALF:P, :], tau_all[HALF:P, :], tau_terms[HALF:P, :], SUBTRACT)
            return tau_terms

        def open_margin(batch):
            size = BATCH_SIZES[batch]
            margin = psum_margin.tile([P, BANK_BLOCKS * KQ], F32, name="margin")
            nc.tensor.matmul(
                margin[:, 0 : size * KQ].rearrange("p (i f) -> p i f", f=KQ),
                lhsT=minus_share[:],
                rhs=tau_terms[:].unsqueeze(1).to_broadcast([P, size, KQ]),
                start=True,
                stop=False,
            )
            return margin

        def compare(team, k, flipped):
            width = TEAM_SIZES[team] * P
            rule = rule_pool.tile([P, BANK_BLOCKS * P], BF16, name="rule")
            bias = 0.0 if k == 0 else shift[:, k : k + 1]
            nc.scalar.activation(
                rule[:, 0:width], flipped[:, 0:width], FUNC.Tanh, scale=steep[:, k : k + 1], bias=bias
            )
            return rule

        def weigh(batch, team, k, rule, margin):
            for i in range(TEAM_SIZES[team]):
                i_batch = TEAM_STARTS[team] + i - BATCH_STARTS[batch]
                nc.tensor.matmul(
                    margin[:, i_batch * KQ + k * Q : i_batch * KQ + (k + 1) * Q],
                    lhsT=rule[:, i * P : (i + 1) * P],
                    rhs=weights[:, k * Q : (k + 1) * Q],
                    start=False,
                    stop=(k == K - 1 and i_batch == BATCH_SIZES[batch] - 1),
                )

        def finish(batch, margin):
            size = BATCH_SIZES[batch]
            active = out_pool.tile([P, BANK_BLOCKS * KQ], F32, name="active")
            nc.scalar.activation(active[:, 0 : size * KQ], margin[:, 0 : size * KQ], FUNC.Sigmoid, scale=6.0)
            nc.sync.dma_start(
                out_view[:, BATCH_STARTS[batch] : BATCH_STARTS[batch] + size, :],
                active[:, 0 : size * KQ].rearrange("p (i f) -> p i f", f=KQ),
            )

        flipped_of = {0: look_up(0)}
        steep, shift = prepare_comparison()
        flipped_of[1] = look_up(1)
        margin_of = {}
        for batch in range(len(BATCHES)):
            rules = {}
            for team in BATCHES[batch]:
                for k in range(K):
                    rules[team, k] = compare(team, k, flipped_of[team])
                    if team == 1 and k == K // 2 - 1:
                        weights = prepare_weights()
                    if batch == len(BATCHES) - 1 and k == K // 2 - 1:
                        finish(0, margin_of[0])
                if team == 0:
                    flipped_of[2] = look_up(2)
                if team == 1:
                    tau_terms = split_tau()
                if batch == len(BATCHES) - 1:
                    finish(batch - 1, margin_of[batch - 1])
            margin_of[batch] = open_margin(batch)
            for team in BATCHES[batch]:
                for k in range(K):
                    weigh(batch, team, k, rules[team, k], margin_of[batch])
            if batch == 0:
                flipped_of[3] = look_up(3)
        finish(len(BATCHES) - 1, margin_of[len(BATCHES) - 1])
